import numpy as np
import ml_dtypes


def mxq(x, axis, fmt="e4m3"):
    dtype, down = {"e4m3": (ml_dtypes.float8_e4m3fn, 7), "e5m2": (ml_dtypes.float8_e5m2, 14)}[fmt]
    v = np.moveaxis(np.asarray(x, np.float32).astype(ml_dtypes.bfloat16).astype(np.float64), axis, -1)
    blocks = v.reshape(v.shape[:-1] + (-1, 32))
    amax = np.abs(blocks).max(-1, keepdims=True)
    byte = np.maximum(np.where(amax > 0, np.frexp(amax)[1] - 1 + 127, 0) - down, 1)
    scale = np.exp2(byte - 127.0)
    codes = (blocks / scale).astype(np.float32).astype(dtype).astype(np.float64)
    return np.moveaxis((codes * scale).reshape(v.shape), -1, axis)


WIDE = False


def mx_kscale(k):
    if not WIDE:
        return np.ones(k)
    levels = np.array([18, -18])
    if k % 512:
        return np.exp2(np.random.permutation(np.resize(levels, k // 32))).repeat(32)
    a = np.empty((k // 512, 16))
    for p in range(k // 512):
        a[p, :8] = np.random.permutation(np.resize(levels, 8))
        for g in range(8):
            far = levels[np.abs(levels - a[p, g]) >= 10]
            a[p, g + 8] = far[np.random.randint(len(far))]
    return np.exp2(a.ravel()).repeat(32)


BF16 = ml_dtypes.bfloat16


def bf(x):
    return np.asarray(x, np.float32).astype(BF16)


def f64(x):
    return np.asarray(x).astype(np.float64)


B, CI, CO, H, W = 4, 1024, 1024, 32, 32
HP, WP = H // 2, W // 2
T = B * HP * WP
EPS = 1e-5


def affine(gamma, beta, running_mean, running_var):
    scale = f64(gamma) / np.sqrt(f64(running_var) + EPS)
    shift = f64(beta) - f64(running_mean) * scale
    return scale, shift


def up2(v):
    return np.repeat(np.repeat(v, 2, axis=-2), 2, axis=-1)


def pool2(r):
    return r.reshape(B, CI, HP, 2, WP, 2).mean(axis=(3, 5))


def setup_inputs():
    s = mx_kscale(T).reshape(B, 1, HP, WP)
    u = mx_kscale(CO)
    m = np.min(s)
    x0 = f64(bf(np.random.standard_normal((B, CI, H, W))))
    gamma = bf(0.5 + np.random.random(CI))
    beta0 = bf(np.random.standard_normal(CI) * 0.5)
    mean0 = bf(np.random.standard_normal(CI) * 0.5)
    running_var = bf(0.5 + np.random.random(CI))
    w0 = bf(np.random.standard_normal((CO, CI, 1, 1)) * 1.5 / np.sqrt(CI))
    scale, shift = affine(gamma, beta0, mean0, running_var)
    xn = x0 * scale[None, :, None, None] + shift[None, :, None, None]
    x0 = f64(bf(np.where(np.abs(xn) < 1e-3, x0 + 0.0625, x0)))
    g = (np.random.standard_normal((B, CO, HP, WP)) * 4.0
         * np.exp2(np.random.randint(-6, 1, (B, 1, HP, WP))))
    return {"x": bf(x0 * up2(s)),
            "gamma": gamma,
            "beta": bf(f64(beta0) * m),
            "running_mean": bf(f64(mean0) * m),
            "running_var": running_var,
            "weight": bf(f64(w0) / u[:, None, None, None]),
            "grad_out": bf(g / s * u[None, :, None, None])}


def reference(x, gamma, beta, running_mean, running_var, weight, grad_out):
    scale, shift = affine(gamma, beta, running_mean, running_var)
    xn = f64(x) * scale[None, :, None, None] + shift[None, :, None, None]
    p = pool2(np.maximum(xn, 0.0)).transpose(1, 0, 2, 3).reshape(CI, T)
    g = f64(grad_out).transpose(1, 0, 2, 3).reshape(CO, T)
    w2d = f64(weight).reshape(CO, CI)
    dp = mxq(w2d, 0, "e4m3").T @ mxq(g, 0, "e5m2")
    dp = dp.reshape(CI, B, HP, WP).transpose(1, 0, 2, 3)
    dx = np.where(xn > 0.0, 0.25 * up2(dp), 0.0) * scale[None, :, None, None]
    dw = mxq(g, 1, "e5m2") @ mxq(p, 1, "e4m3").T
    return dx, dw.reshape(CO, CI, 1, 1)

@@ -1,0 +1,347 @@
+from contextlib import ExitStack
+
+import concourse.mybir as mybir
+from concourse.masks import make_identity
+
+F32 = mybir.dt.float32
+BF16 = mybir.dt.bfloat16
+U32 = mybir.dt.uint32
+U8 = mybir.dt.uint8
+E4M3 = mybir.dt.float8_e4m3fn_x4
+E5M2 = mybir.dt.float8_e5m2_x4
+ALU = mybir.AluOpType
+ACT = mybir.ActivationFunctionType
+
+FLOPS = 2 * 2 * 1024 * 1024 * 1024
+EPS = 1e-5
+P = 128
+
+
+def tile_modelnew_v_kernel(tc, x, gamma, beta, running_mean, running_var, weight, grad_out, out_0, out_1):
+    nc = tc.nc
+    with ExitStack() as ctx:
+        const = ctx.enter_context(tc.tile_pool(name="const", bufs=1))
+        big = ctx.enter_context(tc.tile_pool(name="big", bufs=9))
+        grp = ctx.enter_context(tc.tile_pool(name="grp", bufs=5))
+        codes = ctx.enter_context(tc.tile_pool(name="codes", bufs=1))
+        mkp = ctx.enter_context(tc.tile_pool(name="mkp", bufs=8))
+        rpool = ctx.enter_context(tc.tile_pool(name="rpool", bufs=4))
+        pgp = ctx.enter_context(tc.tile_pool(name="pgp", bufs=4))
+        o0p = ctx.enter_context(tc.tile_pool(name="o0p", bufs=4))
+        o1p = ctx.enter_context(tc.tile_pool(name="o1p", bufs=3))
+        ps_dp = ctx.enter_context(tc.psum_pool(name="ps_dp", bufs=2))
+        ps_pt = ctx.enter_context(tc.psum_pool(name="ps_pt", bufs=2))
+        ps_mm = ctx.enter_context(tc.psum_pool(name="ps_mm", bufs=4))
+
+        raw = {}
+        ggrp = {}
+        wgrp = {}
+        gtgrp = {}
+        gcodes = {}
+        wcodes = {}
+        gtcodes = {}
+        pcodes = {}
+        rt = {}
+        mk = {}
+        dps = {}
+        pts = {}
+        pgs = {}
+        o0 = {}
+        o1 = {}
+
+        def code_pair(name, n):
+            c = codes.tile([P, n], U32, name=name + "_c", align_bytes=256)
+            s = codes.tile([P, n], U8, name=name + "_s", align_bytes=256)
+            return (c, s)
+
+        def load_g(h):
+            t = big.tile([P, 4096], BF16, name="big", align_bytes=256)
+            for G in range(2):
+                nc.sync.dma_start(
+                    out=t[:, G * 2048 : (G + 1) * 2048].rearrange("p (b f) -> p b f", b=2),
+                    in_=grad_out[2 * h : 2 * h + 2, 512 * G : 512 * G + 512, :, :].rearrange("b (p j) y z -> p b (j y z)", j=4),
+                )
+            raw["g", h] = t
+
+        def load_w(G):
+            t = big.tile([P, 4096], BF16, name="big", align_bytes=256)
+            nc.sync.dma_start(out=t[:], in_=weight[512 * G : 512 * G + 512, :, :, :].rearrange("(p j) c u v -> p (j c u v)", j=4))
+            raw["w", G] = t
+
+        def load_x(b, Q):
+            t = big.tile([P, 4096], BF16, name="big", align_bytes=256)
+            nc.sync.dma_start(out=t[:], in_=x[b, 512 * Q : 512 * Q + 512, :, :].rearrange("(p j) y z -> p (j y z)", j=4))
+            raw["x", b, Q] = t
+
+        def g_inter(h, G):
+            t = grp.tile([P, 2048], BF16, name="grp", align_bytes=256)
+            nc.vector.tensor_copy(
+                out=t[:].rearrange("p (b k j) -> p b k j", b=2, j=4),
+                in_=raw["g", h][:, G * 2048 : (G + 1) * 2048].rearrange("p (b j k) -> p b k j", b=2, j=4),
+            )
+            ggrp[h, G] = t
+
+        def g_quant(h, G):
+            c, s = code_pair("gc%d%d" % (h, G), 512)
+            nc.vector.quantize_mx(out=c[:].bitcast(E5M2), scales=s[:], in_=ggrp[h, G][:])
+            gcodes[h, G] = (c, s)
+
+        def g_transpose(h, G, eng):
+            t = grp.tile([P, 2048], BF16, name="grp", align_bytes=256)
+            view = ggrp[h, G][:].rearrange("p (k t j) -> p t j k", t=4, j=4)
+            for jo in range(4):
+                ps = ps_mm.tile([P, 4, P], BF16, name="mm")
+                for tt in range(4):
+                    nc.tensor.transpose(ps[:, tt, :], view[:, tt, jo, :], ident_b[:])
+                eng(t[:, jo * 512 : (jo + 1) * 512].rearrange("p (m t) -> p m t", t=4), ps[:].rearrange("p t m -> p m t"))
+            gtgrp[h, G] = t
+
+        def gt_quant(h, G):
+            c, s = code_pair("tc%d%d" % (h, G), 512)
+            nc.vector.quantize_mx(out=c[:].bitcast(E5M2), scales=s[:], in_=gtgrp[h, G][:])
+            gtcodes[h, G] = (c, s)
+
+        def w_inter(G, Q):
+            t = grp.tile([P, 2048], BF16, name="grp", align_bytes=256)
+            src = raw["w", G][:].rearrange("p (o c) -> p o c", o=4)[:, :, 512 * Q : 512 * Q + 512]
+            nc.vector.tensor_copy(
+                out=t[:].rearrange("p (j m o) -> p j m o", j=4, o=4),
+                in_=src.rearrange("p o (m j) -> p j m o", j=4),
+            )
+            wgrp[G, Q] = t
+
+        def w_quant(G, Q):
+            c, s = code_pair("wc%d%d" % (G, Q), 512)
+            nc.vector.quantize_mx(out=c[:].bitcast(E4M3), scales=s[:], in_=wgrp[G, Q][:])
+            wcodes[G, Q] = (c, s)
+
+        def mask(u, im):
+            Q, h, j = u
+            t = mkp.tile([P, 1024], BF16, name="mask", align_bytes=64)
+            q = 4 * Q + j
+            nc.vector.tensor_scalar(
+                out=t[:],
+                in0=raw["x", 2 * h + im, Q][:, j * 1024 : (j + 1) * 1024],
+                scalar1=s4[:, q : q + 1],
+                scalar2=nb4[:, q : q + 1],
+                op0=ALU.mult,
+                op1=ALU.is_gt,
+            )
+            mk[u, im] = t
+
+        def act(u, im):
+            Q, h, j = u
+            q = 4 * Q + j
+            if im == 0:
+                rt[u] = rpool.tile([P, 2, 2, 512], F32, name="r", align_bytes=64)
+            nc.scalar.activation(
+                out=rt[u][:, :, im, :].rearrange("p d (i z) -> p d i z", z=32),
+                in_=raw["x", 2 * h + im, Q][:, j * 1024 : (j + 1) * 1024].rearrange("p (i d z) -> p d i z", d=2, z=32),
+                func=ACT.Relu,
+                bias=b4[:, q : q + 1],
+                scale=s4[:, q : q + 1],
+            )
+
+        def p_transpose(u):
+            ps = ps_pt.tile([P, 4, P], F32, name="pt")
+            for t in range(4):
+                for n in range(4):
+                    nc.tensor.matmul(
+                        out=ps[:, t, :],
+                        lhsT=rt[u][:, n // 2, :, :].rearrange("p b (k s) -> p s (b k)", s=8)[:, 2 * t + n % 2, :],
+                        rhs=ident_f[:],
+                        start=(n == 0),
+                        stop=(n == 3),
+                        is_transpose=True,
+                    )
+            pts[u] = ps
+
+        def p_evac(u):
+            t = pgp.tile([P, 512], BF16, name="pg", align_bytes=256)
+            nc.scalar.copy(out=t[:].rearrange("p (m t) -> p m t", t=4), in_=pts[u][:].rearrange("p t m -> p m t"))
+            pgs[u] = t
+
+        def p_quant(u):
+            Q, h, j = u
+            if (h, Q) not in pcodes:
+                pcodes[h, Q] = code_pair("pc%d%d" % (h, Q), 512)
+            c, s = pcodes[h, Q]
+            cols = slice(j * P, (j + 1) * P)
+            nc.vector.quantize_mx(out=c[:, cols].bitcast(E4M3), scales=s[:, cols], in_=pgs[u][:])
+
+        def dp(u):
+            Q, h, j = u
+            ps = ps_dp.tile([P, 512], F32, name="dp")
+            cols = slice(j * P, (j + 1) * P)
+            for G in range(2):
+                wc, ws = wcodes[G, Q]
+                gc, gs = gcodes[h, G]
+                nc.tensor.matmul_mx(
+                    out=ps[:],
+                    lhsT=wc[:, cols].bitcast(E4M3),
+                    lhsT_scale=ws[:, cols],
+                    rhs=gc[:].bitcast(E5M2),
+                    rhs_scale=gs[:],
+                    start=(G == 0),
+                    stop=(G == 1),
+                )
+            dps[u] = ps
+
+        def c_out(u):
+            Q, h, j = u
+            q = 4 * Q + j
+            jp = j // 2
+            for im in range(2):
+                if j % 2 == 0:
+                    o0[Q, h, jp, im] = o0p.tile([P, 2, 1024], F32, name="o0", align_bytes=64)
+                ot = o0[Q, h, jp, im]
+                src = dps[u][:, im * 256 : (im + 1) * 256].rearrange("p (i z) -> p i z", z=16).unsqueeze(3).broadcast_to([P, 16, 16, 2])
+                dst = ot[:, j % 2, :].rearrange("p (i d z w) -> p d i z w", d=2, z=16, w=2)
+                msk = mk[u, im][:].rearrange("p (i d z w) -> p d i z w", d=2, z=16, w=2)
+                for d in range(2):
+                    nc.vector.scalar_tensor_tensor(
+                        out=dst[:, d, :, :, :],
+                        in0=src,
+                        scalar=s4[:, q : q + 1],
+                        in1=msk[:, d, :, :, :],
+                        op0=ALU.mult,
+                        op1=ALU.mult,
+                    )
+                if j % 2 == 1:
+                    nc.sync.dma_start(
+                        out=out_0[2 * h + im, 512 * Q : 512 * Q + 512, :, :].rearrange("(p j) y z -> p j (y z)", j=4)[:, 2 * jp : 2 * jp + 2, :],
+                        in_=ot[:],
+                    )
+
+        def out1(Q, G, jo, eng):
+            ps = ps_mm.tile([P, 512], F32, name="mm")
+            cols = slice(jo * P, (jo + 1) * P)
+            for h in range(2):
+                tcd, tsc = gtcodes[h, G]
+                pc, psc = pcodes[h, Q]
+                nc.tensor.matmul_mx(
+                    out=ps[:],
+                    lhsT=tcd[:, cols].bitcast(E5M2),
+                    lhsT_scale=tsc[:, cols],
+                    rhs=pc[:].bitcast(E4M3),
+                    rhs_scale=psc[:],
+                    start=(h == 0),
+                    stop=(h == 1),
+                )
+            if jo % 2 == 0:
+                o1[Q, G, jo // 2] = o1p.tile([P, 2, 512], F32, name="o1", align_bytes=64)
+            ot = o1[Q, G, jo // 2]
+            eng(ot[:, jo % 2, :].rearrange("p (m j) -> p m j", j=4), ps[:].rearrange("p (j m) -> p m j", j=4))
+            if jo % 2 == 1:
+                nc.sync.dma_start(
+                    out=out_1[512 * G : 512 * G + 512, 512 * Q : 512 * Q + 512, :, :].rearrange("(p j) c u v -> p j (c u v)", j=4)[:, jo - 1 : jo + 1, :],
+                    in_=ot[:],
+                )
+
+        def scopy(o, i):
+            nc.scalar.copy(out=o, in_=i)
+
+        def vcopy(o, i):
+            nc.vector.tensor_copy(out=o, in_=i)
+
+        units = [(Q, h, j) for Q in range(2) for h in range(2) for j in range(4)]
+        N = len(units)
+
+        with tc.manual_schedule():
+            pv = {}
+            for nm, ap in (("var", running_var), ("gamma", gamma), ("mean", running_mean), ("beta", beta)):
+                t = const.tile([P, 2, 4], BF16, name="pv_" + nm)
+                nc.scalar.dma_start(out=t[:], in_=ap.rearrange("(q p j) -> p q j", q=2, j=4))
+                pv[nm] = t[:].rearrange("p q j -> p (q j)")
+            load_g(0)
+            load_x(0, 0)
+            load_w(0)
+            load_w(1)
+            load_x(1, 0)
+            load_g(1)
+            load_x(2, 0)
+            load_x(3, 0)
+            for b in range(4):
+                load_x(b, 1)
+
+            ident_f = const.tile([P, P], F32, name="ident_f", align_bytes=64)
+            ident_b = const.tile([P, P], BF16, name="ident_b", align_bytes=64)
+            make_identity(nc, ident_b[:])
+            make_identity(nc, ident_f[:])
+            ve = const.tile([P, 8], F32, name="ve")
+            sd = const.tile([P, 8], F32, name="sd")
+            rs = const.tile([P, 8], F32, name="rs")
+            s4 = const.tile([P, 8], F32, name="s4")
+            ms = const.tile([P, 8], F32, name="ms")
+            b4 = const.tile([P, 8], F32, name="b4")
+            nb4 = const.tile([P, 8], F32, name="nb4")
+            warm = const.tile([P, 8], F32, name="warm")
+            nc.vector.memset(warm[:], 1.0)
+            nc.scalar.activation(out=sd[:], in_=warm[:], func=ACT.Sqrt)
+            nc.vector.tensor_scalar(out=ve[:], in0=pv["var"], scalar1=EPS, scalar2=None, op0=ALU.add)
+            nc.scalar.activation(out=sd[:], in_=ve[:], func=ACT.Sqrt)
+            nc.vector.reciprocal(out=rs[:], in_=sd[:])
+            nc.vector.scalar_tensor_tensor(out=s4[:], in0=pv["gamma"], scalar=0.25, in1=rs[:], op0=ALU.mult, op1=ALU.mult)
+            nc.vector.tensor_tensor(out=ms[:], in0=pv["mean"], in1=s4[:], op=ALU.mult)
+            nc.vector.scalar_tensor_tensor(out=b4[:], in0=pv["beta"], scalar=0.25, in1=ms[:], op0=ALU.mult, op1=ALU.subtract)
+            nc.vector.tensor_scalar(out=nb4[:], in0=b4[:], scalar1=-1.0, scalar2=None, op0=ALU.mult)
+
+            g_inter(0, 0)
+            g_inter(0, 1)
+            g_transpose(0, 0, scopy)
+            g_quant(0, 0)
+            g_quant(0, 1)
+            g_transpose(0, 1, scopy)
+            for j in range(4):
+                act(units[j], 0)
+            mask(units[0], 0)
+            mask(units[1], 0)
+            w_inter(0, 0)
+            w_inter(1, 0)
+            gt_quant(0, 0)
+            w_quant(0, 0)
+            w_quant(1, 0)
+            gt_quant(0, 1)
+            dp(units[0])
+            mask(units[0], 1)
+            mask(units[1], 1)
+            for n in range(N + 3):
+                if n < N:
+                    if n >= 4:
+                        act(units[n], 0)
+                    act(units[n], 1)
+                if 1 <= n <= N:
+                    p_transpose(units[n - 1])
+                    p_evac(units[n - 1])
+                if n + 1 < N:
+                    dp(units[n + 1])
+                if n < N:
+                    if n + 2 < N:
+                        if n == 2:
+                            g_inter(1, 0)
+                            g_inter(1, 1)
+                            g_quant(1, 0)
+                            g_quant(1, 1)
+                        mask(units[n + 2], 0)
+                        mask(units[n + 2], 1)
+                    c_out(units[n])
+                if 2 <= n <= N + 1:
+                    p_quant(units[n - 2])
+                if n == 1:
+                    w_inter(0, 1)
+                    w_inter(1, 1)
+                    w_quant(0, 1)
+                    w_quant(1, 1)
+                if n == 4:
+                    g_transpose(1, 0, scopy)
+                if n == 5:
+                    g_transpose(1, 1, scopy)
+                    gt_quant(1, 0)
+                if n == 6:
+                    gt_quant(1, 1)
+                if 10 <= n < 14:
+                    for e in range(2):
+                        i = 2 * (n - 10) + e
+                        out1(0, i // 4, i % 4, scopy)
+            for i in range(8):
+                out1(1, i // 4, i % 4, (scopy, vcopy)[i % 2])

@@ -21,11 +21,12 @@ def tile_modelnew_v_kernel(tc, x, gamma, beta, running_mean, running_var, weight
     nc = tc.nc
     with ExitStack() as ctx:
         const = ctx.enter_context(tc.tile_pool(name="const", bufs=1))
-        big = ctx.enter_context(tc.tile_pool(name="big", bufs=9))
+        xp = ctx.enter_context(tc.tile_pool(name="xp", bufs=3))
+        rawp = ctx.enter_context(tc.tile_pool(name="rawp", bufs=3))
         grp = ctx.enter_context(tc.tile_pool(name="grp", bufs=5))
         codes = ctx.enter_context(tc.tile_pool(name="codes", bufs=1))
-        mkp = ctx.enter_context(tc.tile_pool(name="mkp", bufs=8))
-        rpool = ctx.enter_context(tc.tile_pool(name="rpool", bufs=4))
+        mkp = ctx.enter_context(tc.tile_pool(name="mkp", bufs=4))
+        rpool = ctx.enter_context(tc.tile_pool(name="rpool", bufs=3))
         pgp = ctx.enter_context(tc.tile_pool(name="pgp", bufs=4))
         o0p = ctx.enter_context(tc.tile_pool(name="o0p", bufs=4))
         o1p = ctx.enter_context(tc.tile_pool(name="o1p", bufs=3))
@@ -55,7 +56,7 @@ def tile_modelnew_v_kernel(tc, x, gamma, beta, running_mean, running_var, weight
             return (c, s)
 
         def load_g(h):
-            t = big.tile([P, 4096], BF16, name="big", align_bytes=256)
+            t = rawp.tile([P, 4096], BF16, name="rawt", align_bytes=256)
             for G in range(2):
                 nc.sync.dma_start(
                     out=t[:, G * 2048 : (G + 1) * 2048].rearrange("p (b f) -> p b f", b=2),
@@ -64,21 +65,25 @@ def tile_modelnew_v_kernel(tc, x, gamma, beta, running_mean, running_var, weight
             raw["g", h] = t
 
         def load_w(G):
-            t = big.tile([P, 4096], BF16, name="big", align_bytes=256)
+            t = rawp.tile([P, 4096], BF16, name="rawt", align_bytes=256)
             nc.sync.dma_start(out=t[:], in_=weight[512 * G : 512 * G + 512, :, :, :].rearrange("(p j) c u v -> p (j c u v)", j=4))
             raw["w", G] = t
 
-        def load_x(b, Q):
-            t = big.tile([P, 4096], BF16, name="big", align_bytes=256)
-            nc.sync.dma_start(out=t[:], in_=x[b, 512 * Q : 512 * Q + 512, :, :].rearrange("(p j) y z -> p (j y z)", j=4))
-            raw["x", b, Q] = t
+        def load_x(h, Q):
+            t = xp.tile([P, 4, 2, 1024], BF16, name="xt", align_bytes=256)
+            for im in range(2):
+                nc.sync.dma_start(
+                    out=t[:, :, im, :],
+                    in_=x[2 * h + im, 512 * Q : 512 * Q + 512, :, :].rearrange("(p j) y z -> p j (y z)", j=4),
+                )
+            raw["x", h, Q] = t
 
         def g_inter(h, G):
             t = grp.tile([P, 2048], BF16, name="grp", align_bytes=256)
-            nc.vector.tensor_copy(
-                out=t[:].rearrange("p (b k j) -> p b k j", b=2, j=4),
-                in_=raw["g", h][:, G * 2048 : (G + 1) * 2048].rearrange("p (b j k) -> p b k j", b=2, j=4),
-            )
+            dst = t[:].rearrange("p (i b m z j) -> p i b m z j", i=2, b=2, m=8, j=4)
+            src = raw["g", h][:, G * 2048 : (G + 1) * 2048].rearrange("p (b j m i z) -> p i b m z j", b=2, j=4, m=8, i=2)
+            for i in range(2):
+                nc.vector.tensor_copy(out=dst[:, i, :, :, :, :], in_=src[:, i, :, :, :, :])
             ggrp[h, G] = t
 
         def g_quant(h, G):
@@ -88,11 +93,11 @@ def tile_modelnew_v_kernel(tc, x, gamma, beta, running_mean, running_var, weight
 
         def g_transpose(h, G, eng):
             t = grp.tile([P, 2048], BF16, name="grp", align_bytes=256)
-            view = ggrp[h, G][:].rearrange("p (k t j) -> p t j k", t=4, j=4)
+            view = ggrp[h, G][:].rearrange("p (i k e j) -> p i e j k", i=2, e=2, j=4)
             for jo in range(4):
                 ps = ps_mm.tile([P, 4, P], BF16, name="mm")
                 for tt in range(4):
-                    nc.tensor.transpose(ps[:, tt, :], view[:, tt, jo, :], ident_b[:])
+                    nc.tensor.transpose(ps[:, tt, :], view[:, tt // 2, tt % 2, jo, :], ident_b[:])
                 eng(t[:, jo * 512 : (jo + 1) * 512].rearrange("p (m t) -> p m t", t=4), ps[:].rearrange("p t m -> p m t"))
             gtgrp[h, G] = t
 
@@ -115,32 +120,34 @@ def tile_modelnew_v_kernel(tc, x, gamma, beta, running_mean, running_var, weight
             nc.vector.quantize_mx(out=c[:].bitcast(E4M3), scales=s[:], in_=wgrp[G, Q][:])
             wcodes[G, Q] = (c, s)
 
-        def mask(u, im):
+        def mask(u):
             Q, h, j = u
-            t = mkp.tile([P, 1024], BF16, name="mask", align_bytes=64)
+            t = mkp.tile([P, 2048], BF16, name="mask", align_bytes=64)
             q = 4 * Q + j
             nc.vector.tensor_scalar(
                 out=t[:],
-                in0=raw["x", 2 * h + im, Q][:, j * 1024 : (j + 1) * 1024],
+                in0=raw["x", h, Q][:, j, :, :].rearrange("p b f -> p (b f)"),
                 scalar1=s4[:, q : q + 1],
                 scalar2=nb4[:, q : q + 1],
                 op0=ALU.mult,
                 op1=ALU.is_gt,
             )
-            mk[u, im] = t
+            mk[u] = t
 
-        def act(u, im):
+        def act(u):
             Q, h, j = u
             q = 4 * Q + j
-            if im == 0:
-                rt[u] = rpool.tile([P, 2, 2, 512], F32, name="r", align_bytes=64)
-            nc.scalar.activation(
-                out=rt[u][:, :, im, :].rearrange("p d (i z) -> p d i z", z=32),
-                in_=raw["x", 2 * h + im, Q][:, j * 1024 : (j + 1) * 1024].rearrange("p (i d z) -> p d i z", d=2, z=32),
-                func=ACT.Relu,
-                bias=b4[:, q : q + 1],
-                scale=s4[:, q : q + 1],
-            )
+            t = rpool.tile([P, 4, 4, P], F32, name="r", align_bytes=64)
+            src = raw["x", h, Q][:, j, :, :].rearrange("p b (m c k e) -> p e (b m) c k", m=8, c=4, e=4)
+            for e in range(4):
+                nc.scalar.activation(
+                    out=t[:, e, :, :].rearrange("p c (g k) -> p g c k", k=8),
+                    in_=src[:, e, :, :, :],
+                    func=ACT.Relu,
+                    bias=b4[:, q : q + 1],
+                    scale=s4[:, q : q + 1],
+                )
+            rt[u] = t
 
         def p_transpose(u):
             ps = ps_pt.tile([P, 4, P], F32, name="pt")
@@ -148,7 +155,7 @@ def tile_modelnew_v_kernel(tc, x, gamma, beta, running_mean, running_var, weight
                 for n in range(4):
                     nc.tensor.matmul(
                         out=ps[:, t, :],
-                        lhsT=rt[u][:, n // 2, :, :].rearrange("p b (k s) -> p s (b k)", s=8)[:, 2 * t + n % 2, :],
+                        lhsT=rt[u][:, 2 * (t % 2) + n % 2, 2 * (t // 2) + n // 2, :],
                         rhs=ident_f[:],
                         start=(n == 0),
                         stop=(n == 3),
@@ -190,28 +197,24 @@ def tile_modelnew_v_kernel(tc, x, gamma, beta, running_mean, running_var, weight
         def c_out(u):
             Q, h, j = u
             q = 4 * Q + j
-            jp = j // 2
-            for im in range(2):
-                if j % 2 == 0:
-                    o0[Q, h, jp, im] = o0p.tile([P, 2, 1024], F32, name="o0", align_bytes=64)
-                ot = o0[Q, h, jp, im]
-                src = dps[u][:, im * 256 : (im + 1) * 256].rearrange("p (i z) -> p i z", z=16).unsqueeze(3).broadcast_to([P, 16, 16, 2])
-                dst = ot[:, j % 2, :].rearrange("p (i d z w) -> p d i z w", d=2, z=16, w=2)
-                msk = mk[u, im][:].rearrange("p (i d z w) -> p d i z w", d=2, z=16, w=2)
+            ot = o0p.tile([P, 2048], F32, name="o0", align_bytes=64)
+            dst = ot[:].rearrange("p (g i d z w) -> p i d g z w", i=2, d=2, z=16, w=2)
+            msk = mk[u][:].rearrange("p (g i d z w) -> p i d g z w", i=2, d=2, z=16, w=2)
+            for i in range(2):
+                src = dps[u][:, i * 256 : (i + 1) * 256].rearrange("p (g z) -> p g z", z=16).unsqueeze(3).broadcast_to([P, 16, 16, 2])
                 for d in range(2):
                     nc.vector.scalar_tensor_tensor(
-                        out=dst[:, d, :, :, :],
+                        out=dst[:, i, d, :, :, :],
                         in0=src,
                         scalar=s4[:, q : q + 1],
-                        in1=msk[:, d, :, :, :],
+                        in1=msk[:, i, d, :, :, :],
                         op0=ALU.mult,
                         op1=ALU.mult,
                     )
-                if j % 2 == 1:
-                    nc.sync.dma_start(
-                        out=out_0[2 * h + im, 512 * Q : 512 * Q + 512, :, :].rearrange("(p j) y z -> p j (y z)", j=4)[:, 2 * jp : 2 * jp + 2, :],
-                        in_=ot[:],
-                    )
+            nc.sync.dma_start(
+                out=out_0[2 * h : 2 * h + 2, 512 * Q : 512 * Q + 512, :, :].rearrange("b (p j) y z -> p j b (y z)", j=4)[:, j, :, :],
+                in_=ot[:].rearrange("p (b f) -> p b f", b=2),
+            )
 
         def out1(Q, G, jo, eng):
             ps = ps_mm.tile([P, 512], F32, name="mm")
@@ -257,17 +260,18 @@ def tile_modelnew_v_kernel(tc, x, gamma, beta, running_mean, running_var, weight
             load_x(0, 0)
             load_w(0)
             load_w(1)
-            load_x(1, 0)
             load_g(1)
-            load_x(2, 0)
-            load_x(3, 0)
-            for b in range(4):
-                load_x(b, 1)
+            load_x(1, 0)
+            load_x(0, 1)
+            load_x(1, 1)
 
             ident_f = const.tile([P, P], F32, name="ident_f", align_bytes=64)
             ident_b = const.tile([P, P], BF16, name="ident_b", align_bytes=64)
             make_identity(nc, ident_b[:])
             make_identity(nc, ident_f[:])
+            g_inter(0, 0)
+            g_inter(0, 1)
+            g_transpose(0, 0, scopy)
             ve = const.tile([P, 8], F32, name="ve")
             sd = const.tile([P, 8], F32, name="sd")
             rs = const.tile([P, 8], F32, name="rs")
@@ -286,62 +290,152 @@ def tile_modelnew_v_kernel(tc, x, gamma, beta, running_mean, running_var, weight
             nc.vector.scalar_tensor_tensor(out=b4[:], in0=pv["beta"], scalar=0.25, in1=ms[:], op0=ALU.mult, op1=ALU.subtract)
             nc.vector.tensor_scalar(out=nb4[:], in0=b4[:], scalar1=-1.0, scalar2=None, op0=ALU.mult)
 
-            g_inter(0, 0)
-            g_inter(0, 1)
-            g_transpose(0, 0, scopy)
+            g_transpose(0, 1, scopy)
             g_quant(0, 0)
             g_quant(0, 1)
-            g_transpose(0, 1, scopy)
-            for j in range(4):
-                act(units[j], 0)
-            mask(units[0], 0)
-            mask(units[1], 0)
-            w_inter(0, 0)
-            w_inter(1, 0)
+            mask(units[0])
+            mask(units[1])
             gt_quant(0, 0)
+            w_inter(0, 0)
+            gt_quant(0, 1)
+            w_inter(1, 0)
             w_quant(0, 0)
             w_quant(1, 0)
-            gt_quant(0, 1)
             dp(units[0])
-            mask(units[0], 1)
-            mask(units[1], 1)
-            for n in range(N + 3):
-                if n < N:
-                    if n >= 4:
-                        act(units[n], 0)
-                    act(units[n], 1)
-                if 1 <= n <= N:
-                    p_transpose(units[n - 1])
-                    p_evac(units[n - 1])
-                if n + 1 < N:
-                    dp(units[n + 1])
-                if n < N:
-                    if n + 2 < N:
-                        if n == 2:
-                            g_inter(1, 0)
-                            g_inter(1, 1)
-                            g_quant(1, 0)
-                            g_quant(1, 1)
-                        mask(units[n + 2], 0)
-                        mask(units[n + 2], 1)
-                    c_out(units[n])
-                if 2 <= n <= N + 1:
-                    p_quant(units[n - 2])
-                if n == 1:
-                    w_inter(0, 1)
-                    w_inter(1, 1)
-                    w_quant(0, 1)
-                    w_quant(1, 1)
-                if n == 4:
-                    g_transpose(1, 0, scopy)
-                if n == 5:
-                    g_transpose(1, 1, scopy)
-                    gt_quant(1, 0)
-                if n == 6:
-                    gt_quant(1, 1)
-                if 10 <= n < 14:
-                    for e in range(2):
-                        i = 2 * (n - 10) + e
-                        out1(0, i // 4, i % 4, scopy)
-            for i in range(8):
-                out1(1, i // 4, i % 4, (scopy, vcopy)[i % 2])
+            act(units[0])
+            act(units[1])
+            p_transpose(units[0])
+            p_evac(units[0])
+            dp(units[1])
+            mask(units[2])
+            c_out(units[0])
+            g_inter(1, 0)
+            act(units[2])
+            p_transpose(units[1])
+            p_evac(units[1])
+            dp(units[2])
+            mask(units[3])
+            p_quant(units[0])
+            c_out(units[1])
+            g_inter(1, 1)
+            g_quant(1, 0)
+            act(units[3])
+            p_transpose(units[2])
+            p_evac(units[2])
+            dp(units[3])
+            mask(units[4])
+            p_quant(units[1])
+            c_out(units[2])
+            g_quant(1, 1)
+            g_transpose(1, 0, scopy)
+            act(units[4])
+            p_transpose(units[3])
+            p_evac(units[3])
+            dp(units[4])
+            mask(units[5])
+            p_quant(units[2])
+            c_out(units[3])
+            g_transpose(1, 1, scopy)
+            w_inter(0, 1)
+            act(units[5])
+            p_transpose(units[4])
+            p_evac(units[4])
+            dp(units[5])
+            mask(units[6])
+            p_quant(units[3])
+            c_out(units[4])
+            w_inter(1, 1)
+            gt_quant(1, 0)
+            w_quant(0, 1)
+            act(units[6])
+            p_transpose(units[5])
+            p_evac(units[5])
+            dp(units[6])
+            mask(units[7])
+            p_quant(units[4])
+            c_out(units[5])
+            w_quant(1, 1)
+            gt_quant(1, 1)
+            act(units[7])
+            p_transpose(units[6])
+            p_evac(units[6])
+            dp(units[7])
+            mask(units[8])
+            p_quant(units[5])
+            c_out(units[6])
+            act(units[8])
+            p_transpose(units[7])
+            p_evac(units[7])
+            dp(units[8])
+            mask(units[9])
+            p_quant(units[6])
+            c_out(units[7])
+            act(units[9])
+            p_transpose(units[8])
+            p_evac(units[8])
+            dp(units[9])
+            mask(units[10])
+            p_quant(units[7])
+            c_out(units[8])
+            act(units[10])
+            p_transpose(units[9])
+            p_evac(units[9])
+            dp(units[10])
+            mask(units[11])
+            p_quant(units[8])
+            c_out(units[9])
+            out1(0, 0, 0, scopy)
+            out1(0, 0, 1, scopy)
+            act(units[11])
+            p_transpose(units[10])
+            p_evac(units[10])
+            dp(units[11])
+            mask(units[12])
+            p_quant(units[9])
+            c_out(units[10])
+            out1(0, 0, 2, scopy)
+            out1(0, 0, 3, scopy)
+            act(units[12])
+            p_transpose(units[11])
+            p_evac(units[11])
+            dp(units[12])
+            mask(units[13])
+            p_quant(units[10])
+            c_out(units[11])
+            out1(0, 1, 0, scopy)
+            out1(0, 1, 1, scopy)
+            act(units[13])
+            p_transpose(units[12])
+            p_evac(units[12])
+            dp(units[13])
+            mask(units[14])
+            p_quant(units[11])
+            c_out(units[12])
+            out1(0, 1, 2, scopy)
+            out1(0, 1, 3, scopy)
+            act(units[14])
+            p_transpose(units[13])
+            p_evac(units[13])
+            dp(units[14])
+            mask(units[15])
+            p_quant(units[12])
+            c_out(units[13])
+            act(units[15])
+            p_transpose(units[14])
+            p_evac(units[14])
+            dp(units[15])
+            p_quant(units[13])
+            c_out(units[14])
+            p_transpose(units[15])
+            p_evac(units[15])
+            p_quant(units[14])
+            c_out(units[15])
+            p_quant(units[15])
+            out1(1, 0, 0, scopy)
+            out1(1, 0, 1, vcopy)
+            out1(1, 0, 2, scopy)
+            out1(1, 0, 3, vcopy)
+            out1(1, 1, 0, scopy)
+            out1(1, 1, 1, vcopy)
+            out1(1, 1, 2, scopy)
+            out1(1, 1, 3, vcopy)

@@ -32,7 +32,9 @@ def tile_modelnew_v_kernel(tc, x, gamma, beta, running_mean, running_var, weight
         o1p = ctx.enter_context(tc.tile_pool(name="o1p", bufs=3))
         ps_dp = ctx.enter_context(tc.psum_pool(name="ps_dp", bufs=2))
         ps_pt = ctx.enter_context(tc.psum_pool(name="ps_pt", bufs=2))
-        ps_mm = ctx.enter_context(tc.psum_pool(name="ps_mm", bufs=4))
+        ps_mm = ctx.enter_context(tc.psum_pool(name="ps_mm", bufs=3))
+        ps_warm = ctx.enter_context(tc.psum_pool(name="ps_warm", bufs=1))
+        warm_ps = ps_warm.tile([P, 512], F32, name="warm_ps")
 
         raw = {}
         ggrp = {}
@@ -54,6 +56,12 @@ def tile_modelnew_v_kernel(tc, x, gamma, beta, running_mean, running_var, weight
             c = codes.tile([P, n], U32, name=name + "_c", align_bytes=256)
             s = codes.tile([P, n], U8, name=name + "_s", align_bytes=256)
             return (c, s)
+
+        def scopy(o, i):
+            nc.scalar.copy(out=o, in_=i)
+
+        def vcopy(o, i):
+            nc.vector.tensor_copy(out=o, in_=i)
 
         def load_g(h):
             t = rawp.tile([P, 4096], BF16, name="rawt", align_bytes=256)
@@ -78,12 +86,12 @@ def tile_modelnew_v_kernel(tc, x, gamma, beta, running_mean, running_var, weight
                 )
             raw["x", h, Q] = t
 
-        def g_inter(h, G):
+        def g_inter(h, G, eng=vcopy):
             t = grp.tile([P, 2048], BF16, name="grp", align_bytes=256)
             dst = t[:].rearrange("p (i b m z j) -> p i b m z j", i=2, b=2, m=8, j=4)
             src = raw["g", h][:, G * 2048 : (G + 1) * 2048].rearrange("p (b j m i z) -> p i b m z j", b=2, j=4, m=8, i=2)
             for i in range(2):
-                nc.vector.tensor_copy(out=dst[:, i, :, :, :, :], in_=src[:, i, :, :, :, :])
+                eng(dst[:, i, :, :, :, :], src[:, i, :, :, :, :])
             ggrp[h, G] = t
 
         def g_quant(h, G):
@@ -106,13 +114,10 @@ def tile_modelnew_v_kernel(tc, x, gamma, beta, running_mean, running_var, weight
             nc.vector.quantize_mx(out=c[:].bitcast(E5M2), scales=s[:], in_=gtgrp[h, G][:])
             gtcodes[h, G] = (c, s)
 
-        def w_inter(G, Q):
+        def w_inter(G, Q, eng=vcopy):
             t = grp.tile([P, 2048], BF16, name="grp", align_bytes=256)
             src = raw["w", G][:].rearrange("p (o c) -> p o c", o=4)[:, :, 512 * Q : 512 * Q + 512]
-            nc.vector.tensor_copy(
-                out=t[:].rearrange("p (j m o) -> p j m o", j=4, o=4),
-                in_=src.rearrange("p o (m j) -> p j m o", j=4),
-            )
+            eng(t[:].rearrange("p (j m o) -> p j m o", j=4, o=4), src.rearrange("p o (m j) -> p j m o", j=4))
             wgrp[G, Q] = t
 
         def w_quant(G, Q):
@@ -216,6 +221,10 @@ def tile_modelnew_v_kernel(tc, x, gamma, beta, running_mean, running_var, weight
                 in_=ot[:].rearrange("p (b f) -> p b f", b=2),
             )
 
+        def warm_pe(k, rhs):
+            for i in range(k):
+                nc.tensor.matmul(out=warm_ps[:], lhsT=ident_b[:], rhs=rhs, start=True, stop=True)
+
         def out1(Q, G, jo, eng):
             ps = ps_mm.tile([P, 512], F32, name="mm")
             cols = slice(jo * P, (jo + 1) * P)
@@ -241,37 +250,20 @@ def tile_modelnew_v_kernel(tc, x, gamma, beta, running_mean, running_var, weight
                     in_=ot[:],
                 )
 
-        def scopy(o, i):
-            nc.scalar.copy(out=o, in_=i)
-
-        def vcopy(o, i):
-            nc.vector.tensor_copy(out=o, in_=i)
-
         units = [(Q, h, j) for Q in range(2) for h in range(2) for j in range(4)]
         N = len(units)
 
         with tc.manual_schedule():
             pv = {}
-            for nm, ap in (("var", running_var), ("gamma", gamma), ("mean", running_mean), ("beta", beta)):
-                t = const.tile([P, 2, 4], BF16, name="pv_" + nm)
-                nc.scalar.dma_start(out=t[:], in_=ap.rearrange("(q p j) -> p q j", q=2, j=4))
-                pv[nm] = t[:].rearrange("p q j -> p (q j)")
-            load_g(0)
-            load_x(0, 0)
-            load_w(0)
-            load_w(1)
-            load_g(1)
-            load_x(1, 0)
-            load_x(0, 1)
-            load_x(1, 1)
-
+            def load_params():
+                for nm, ap in (("var", running_var), ("gamma", gamma), ("mean", running_mean), ("beta", beta)):
+                    t = const.tile([P, 2, 4], BF16, name="pv_" + nm)
+                    nc.scalar.dma_start(out=t[:], in_=ap.rearrange("(q p j) -> p q j", q=2, j=4))
+                    pv[nm] = t[:].rearrange("p q j -> p (q j)")
             ident_f = const.tile([P, P], F32, name="ident_f", align_bytes=64)
             ident_b = const.tile([P, P], BF16, name="ident_b", align_bytes=64)
             make_identity(nc, ident_b[:])
             make_identity(nc, ident_f[:])
-            g_inter(0, 0)
-            g_inter(0, 1)
-            g_transpose(0, 0, scopy)
             ve = const.tile([P, 8], F32, name="ve")
             sd = const.tile([P, 8], F32, name="sd")
             rs = const.tile([P, 8], F32, name="rs")
@@ -280,156 +272,188 @@ def tile_modelnew_v_kernel(tc, x, gamma, beta, running_mean, running_var, weight
             b4 = const.tile([P, 8], F32, name="b4")
             nb4 = const.tile([P, 8], F32, name="nb4")
             warm = const.tile([P, 8], F32, name="warm")
+            zero = const.tile([P, 512], BF16, name="zero", align_bytes=64)
+            nc.gpsimd.memset(zero[:], 0.0)
+            def consts():
+                nc.vector.tensor_scalar(out=ve[:], in0=pv["var"], scalar1=EPS, scalar2=None, op0=ALU.add)
+                nc.scalar.activation(out=sd[:], in_=ve[:], func=ACT.Sqrt)
+                nc.vector.reciprocal(out=rs[:], in_=sd[:])
+                nc.vector.scalar_tensor_tensor(out=s4[:], in0=pv["gamma"], scalar=0.25, in1=rs[:], op0=ALU.mult, op1=ALU.mult)
+                nc.vector.tensor_tensor(out=ms[:], in0=pv["mean"], in1=s4[:], op=ALU.mult)
+                nc.vector.scalar_tensor_tensor(out=b4[:], in0=pv["beta"], scalar=0.25, in1=ms[:], op0=ALU.mult, op1=ALU.subtract)
+                nc.vector.tensor_scalar(out=nb4[:], in0=b4[:], scalar1=-1.0, scalar2=None, op0=ALU.mult)
             nc.vector.memset(warm[:], 1.0)
             nc.scalar.activation(out=sd[:], in_=warm[:], func=ACT.Sqrt)
-            nc.vector.tensor_scalar(out=ve[:], in0=pv["var"], scalar1=EPS, scalar2=None, op0=ALU.add)
-            nc.scalar.activation(out=sd[:], in_=ve[:], func=ACT.Sqrt)
-            nc.vector.reciprocal(out=rs[:], in_=sd[:])
-            nc.vector.scalar_tensor_tensor(out=s4[:], in0=pv["gamma"], scalar=0.25, in1=rs[:], op0=ALU.mult, op1=ALU.mult)
-            nc.vector.tensor_tensor(out=ms[:], in0=pv["mean"], in1=s4[:], op=ALU.mult)
-            nc.vector.scalar_tensor_tensor(out=b4[:], in0=pv["beta"], scalar=0.25, in1=ms[:], op0=ALU.mult, op1=ALU.subtract)
-            nc.vector.tensor_scalar(out=nb4[:], in0=b4[:], scalar1=-1.0, scalar2=None, op0=ALU.mult)
-
+            load_params()
+            load_g(0)
+            load_x(0, 0)
+            load_w(0)
+            load_w(1)
+            load_g(1)
+            load_x(1, 0)
+            load_x(0, 1)
+            load_x(1, 1)
+            g_inter(0, 0)
+            g_inter(0, 1)
+            consts()
+            g_quant(0, 1)
             g_transpose(0, 1, scopy)
             g_quant(0, 0)
-            g_quant(0, 1)
-            mask(units[0])
-            mask(units[1])
-            gt_quant(0, 0)
-            w_inter(0, 0)
             gt_quant(0, 1)
-            w_inter(1, 0)
+            g_transpose(0, 0, scopy)
+            mask(units[1])
+            mask(units[0])
+            w_inter(0, 0)
+            gt_quant(0, 0)
             w_quant(0, 0)
+            w_inter(1, 0)
             w_quant(1, 0)
+            warm_pe(4, gtgrp[0, 0][:, 0:512])
             dp(units[0])
             act(units[0])
+            w_inter(0, 1, scopy)
+            g_inter(1, 0, scopy)
+            g_inter(1, 1, vcopy)
             act(units[1])
             p_transpose(units[0])
+            warm_pe(1, zero[:])
             p_evac(units[0])
             dp(units[1])
             mask(units[2])
             c_out(units[0])
-            g_inter(1, 0)
+            g_quant(1, 1)
+            g_quant(1, 0)
             act(units[2])
             p_transpose(units[1])
+            warm_pe(1, zero[:])
             p_evac(units[1])
             dp(units[2])
             mask(units[3])
-            p_quant(units[0])
             c_out(units[1])
-            g_inter(1, 1)
-            g_quant(1, 0)
+            p_quant(units[0])
+            w_inter(1, 1, vcopy)
             act(units[3])
             p_transpose(units[2])
+            warm_pe(1, zero[:])
             p_evac(units[2])
             dp(units[3])
             mask(units[4])
-            p_quant(units[1])
             c_out(units[2])
-            g_quant(1, 1)
-            g_transpose(1, 0, scopy)
+            p_quant(units[1])
+            g_transpose(1, 1, scopy)
             act(units[4])
             p_transpose(units[3])
+            warm_pe(1, zero[:])
             p_evac(units[3])
             dp(units[4])
             mask(units[5])
-            p_quant(units[2])
             c_out(units[3])
-            g_transpose(1, 1, scopy)
-            w_inter(0, 1)
+            p_quant(units[2])
+            w_quant(0, 1)
             act(units[5])
             p_transpose(units[4])
+            warm_pe(1, zero[:])
             p_evac(units[4])
             dp(units[5])
             mask(units[6])
-            p_quant(units[3])
             c_out(units[4])
-            w_inter(1, 1)
-            gt_quant(1, 0)
-            w_quant(0, 1)
+            p_quant(units[3])
             act(units[6])
             p_transpose(units[5])
+            warm_pe(1, zero[:])
             p_evac(units[5])
             dp(units[6])
             mask(units[7])
-            p_quant(units[4])
             c_out(units[5])
-            w_quant(1, 1)
-            gt_quant(1, 1)
+            p_quant(units[4])
             act(units[7])
             p_transpose(units[6])
+            warm_pe(1, zero[:])
             p_evac(units[6])
             dp(units[7])
             mask(units[8])
-            p_quant(units[5])
             c_out(units[6])
+            p_quant(units[5])
+            w_quant(1, 1)
             act(units[8])
             p_transpose(units[7])
+            warm_pe(1, zero[:])
             p_evac(units[7])
             dp(units[8])
             mask(units[9])
-            p_quant(units[6])
             c_out(units[7])
+            p_quant(units[6])
+            g_transpose(1, 0, scopy)
             act(units[9])
             p_transpose(units[8])
+            warm_pe(1, zero[:])
             p_evac(units[8])
             dp(units[9])
             mask(units[10])
-            p_quant(units[7])
             c_out(units[8])
+            p_quant(units[7])
+            gt_quant(1, 0)
             act(units[10])
             p_transpose(units[9])
+            warm_pe(1, zero[:])
             p_evac(units[9])
             dp(units[10])
             mask(units[11])
-            p_quant(units[8])
             c_out(units[9])
+            p_quant(units[8])
+            gt_quant(1, 1)
             out1(0, 0, 0, scopy)
-            out1(0, 0, 1, scopy)
+            out1(0, 0, 1, vcopy)
+            out1(0, 0, 2, scopy)
             act(units[11])
             p_transpose(units[10])
+            warm_pe(1, zero[:])
             p_evac(units[10])
             dp(units[11])
             mask(units[12])
-            p_quant(units[9])
             c_out(units[10])
-            out1(0, 0, 2, scopy)
-            out1(0, 0, 3, scopy)
+            p_quant(units[9])
+            out1(0, 1, 2, vcopy)
+            out1(0, 1, 3, scopy)
             act(units[12])
             p_transpose(units[11])
+            warm_pe(1, zero[:])
             p_evac(units[11])
             dp(units[12])
             mask(units[13])
-            p_quant(units[10])
             c_out(units[11])
-            out1(0, 1, 0, scopy)
-            out1(0, 1, 1, scopy)
+            p_quant(units[10])
+            out1(0, 0, 3, vcopy)
             act(units[13])
             p_transpose(units[12])
+            warm_pe(1, zero[:])
             p_evac(units[12])
             dp(units[13])
             mask(units[14])
-            p_quant(units[11])
             c_out(units[12])
-            out1(0, 1, 2, scopy)
-            out1(0, 1, 3, scopy)
+            p_quant(units[11])
+            out1(0, 1, 0, scopy)
+            out1(0, 1, 1, scopy)
             act(units[14])
             p_transpose(units[13])
+            warm_pe(1, zero[:])
             p_evac(units[13])
             dp(units[14])
             mask(units[15])
-            p_quant(units[12])
             c_out(units[13])
+            p_quant(units[12])
             act(units[15])
             p_transpose(units[14])
+            warm_pe(1, zero[:])
             p_evac(units[14])
             dp(units[15])
-            p_quant(units[13])
             c_out(units[14])
+            p_quant(units[13])
             p_transpose(units[15])
+            warm_pe(1, zero[:])
             p_evac(units[15])
-            p_quant(units[14])
             c_out(units[15])
+            p_quant(units[14])
             p_quant(units[15])
             out1(1, 0, 0, scopy)
             out1(1, 0, 1, vcopy)

@@ -19,447 +19,326 @@ P = 128
 
 def tile_modelnew_v_kernel(tc, x, gamma, beta, running_mean, running_var, weight, grad_out, out_0, out_1):
     nc = tc.nc
+
+    def on_scalar(out, in_):
+        nc.scalar.copy(out=out, in_=in_)
+
+    def on_vector(out, in_):
+        nc.vector.tensor_copy(out=out, in_=in_)
+
+    def on_gpsimd(out, in_):
+        nc.gpsimd.tensor_scalar(out=out, in0=in_, scalar1=1.0, scalar2=0.0, op0=ALU.mult, op1=ALU.add)
+
     with ExitStack() as ctx:
-        const = ctx.enter_context(tc.tile_pool(name="const", bufs=1))
-        xp = ctx.enter_context(tc.tile_pool(name="xp", bufs=3))
-        rawp = ctx.enter_context(tc.tile_pool(name="rawp", bufs=3))
-        grp = ctx.enter_context(tc.tile_pool(name="grp", bufs=5))
-        codes = ctx.enter_context(tc.tile_pool(name="codes", bufs=1))
-        mkp = ctx.enter_context(tc.tile_pool(name="mkp", bufs=4))
-        rpool = ctx.enter_context(tc.tile_pool(name="rpool", bufs=3))
-        pgp = ctx.enter_context(tc.tile_pool(name="pgp", bufs=4))
-        o0p = ctx.enter_context(tc.tile_pool(name="o0p", bufs=4))
-        o1p = ctx.enter_context(tc.tile_pool(name="o1p", bufs=3))
-        ps_dp = ctx.enter_context(tc.psum_pool(name="ps_dp", bufs=2))
-        ps_pt = ctx.enter_context(tc.psum_pool(name="ps_pt", bufs=2))
-        ps_mm = ctx.enter_context(tc.psum_pool(name="ps_mm", bufs=3))
-        ps_warm = ctx.enter_context(tc.psum_pool(name="ps_warm", bufs=1))
-        warm_ps = ps_warm.tile([P, 512], F32, name="warm_ps")
 
-        raw = {}
-        ggrp = {}
-        wgrp = {}
-        gtgrp = {}
-        gcodes = {}
-        wcodes = {}
-        gtcodes = {}
-        pcodes = {}
-        rt = {}
-        mk = {}
-        dps = {}
-        pts = {}
-        pgs = {}
-        o0 = {}
-        o1 = {}
+        def sbuf(name, bufs):
+            return ctx.enter_context(tc.tile_pool(name=name, bufs=bufs))
 
-        def code_pair(name, n):
-            c = codes.tile([P, n], U32, name=name + "_c", align_bytes=256)
-            s = codes.tile([P, n], U8, name=name + "_s", align_bytes=256)
-            return (c, s)
+        def psum(name, bufs):
+            return ctx.enter_context(tc.psum_pool(name=name, bufs=bufs))
 
-        def scopy(o, i):
-            nc.scalar.copy(out=o, in_=i)
+        const = sbuf("const", 1)
+        raw_pool = sbuf("raw_pool", 3)
+        x_pool = sbuf("x_pool", 3)
+        grouped_pool = sbuf("grouped_pool", 5)
+        code_pool = sbuf("code_pool", 1)
+        mask_pool = sbuf("mask_pool", 4)
+        relu_pool = sbuf("relu_pool", 3)
+        pooled_pool = sbuf("pooled_pool", 3)
+        dx_pool = sbuf("dx_pool", 4)
+        dw_pool = sbuf("dw_pool", 4)
+        dp_psum = psum("dp_psum", 3)
+        pool_psum = psum("pool_psum", 2)
+        mix_psum = psum("mix_psum", 3)
 
-        def vcopy(o, i):
-            nc.vector.tensor_copy(out=o, in_=i)
+        raw_g, raw_w, raw_x = {}, {}, {}
+        grouped_g, grouped_w, grouped_gt = {}, {}, {}
+        codes_g, codes_w, codes_gt, codes_p = {}, {}, {}, {}
+        masked, relu, pooled_sum, pooled, dp_sum, dw_tile = {}, {}, {}, {}, {}, {}
+
+        def quantised(name, width, fmt):
+            codes = code_pool.tile([P, width], U32, name=name + "_codes", align_bytes=256)
+            scales = code_pool.tile([P, width], U8, name=name + "_scales", align_bytes=256)
+            return codes, scales, fmt
+
+        def quantise(dst, cols, src):
+            codes, scales, fmt = dst
+            nc.vector.quantize_mx(out=codes[:, cols].bitcast(fmt), scales=scales[:, cols], in_=src)
+
+        def multiply(acc, lhs, lhs_cols, rhs, start, stop):
+            lhs_codes, lhs_scales, lhs_fmt = lhs
+            rhs_codes, rhs_scales, rhs_fmt = rhs
+            nc.tensor.matmul_mx(
+                out=acc,
+                lhsT=lhs_codes[:, lhs_cols].bitcast(lhs_fmt),
+                lhsT_scale=lhs_scales[:, lhs_cols],
+                rhs=rhs_codes[:].bitcast(rhs_fmt),
+                rhs_scale=rhs_scales[:],
+                start=start,
+                stop=stop,
+            )
+
+        everything = slice(0, 512)
+
+        def block(n):
+            return slice(n * P, (n + 1) * P)
+
 
         def load_g(h):
-            t = rawp.tile([P, 4096], BF16, name="rawt", align_bytes=256)
+            t = raw_pool.tile([P, 2, 2, 1024], BF16, name="raw", align_bytes=256)
             for G in range(2):
                 nc.sync.dma_start(
-                    out=t[:, G * 2048 : (G + 1) * 2048].rearrange("p (b f) -> p b f", b=2),
-                    in_=grad_out[2 * h : 2 * h + 2, 512 * G : 512 * G + 512, :, :].rearrange("b (p j) y z -> p b (j y z)", j=4),
+                    out=t[:, G, :, :],
+                    in_=grad_out[2 * h : 2 * h + 2, 512 * G : 512 * G + 512, :, :].rearrange("b (m s) y z -> m b (s y z)", s=4),
                 )
-            raw["g", h] = t
+            raw_g[h] = t
 
         def load_w(G):
-            t = rawp.tile([P, 4096], BF16, name="rawt", align_bytes=256)
-            nc.sync.dma_start(out=t[:], in_=weight[512 * G : 512 * G + 512, :, :, :].rearrange("(p j) c u v -> p (j c u v)", j=4))
-            raw["w", G] = t
+            t = raw_pool.tile([P, 4, 1024], BF16, name="raw", align_bytes=256)
+            nc.sync.dma_start(out=t[:], in_=weight[512 * G : 512 * G + 512, :, :, :].rearrange("(m s) c u v -> m s (c u v)", s=4))
+            raw_w[G] = t
 
         def load_x(h, Q):
-            t = xp.tile([P, 4, 2, 1024], BF16, name="xt", align_bytes=256)
-            for im in range(2):
+            t = x_pool.tile([P, 4, 2, 1024], BF16, name="x_tile", align_bytes=256)
+            for b in range(2):
                 nc.sync.dma_start(
-                    out=t[:, :, im, :],
-                    in_=x[2 * h + im, 512 * Q : 512 * Q + 512, :, :].rearrange("(p j) y z -> p j (y z)", j=4),
+                    out=t[:, :, b, :],
+                    in_=x[2 * h + b, 512 * Q : 512 * Q + 512, :, :].rearrange("(m j) y z -> m j (y z)", j=4),
                 )
-            raw["x", h, Q] = t
+            raw_x[h, Q] = t
 
-        def g_inter(h, G, eng=vcopy):
-            t = grp.tile([P, 2048], BF16, name="grp", align_bytes=256)
-            dst = t[:].rearrange("p (i b m z j) -> p i b m z j", i=2, b=2, m=8, j=4)
-            src = raw["g", h][:, G * 2048 : (G + 1) * 2048].rearrange("p (b j m i z) -> p i b m z j", b=2, j=4, m=8, i=2)
-            for i in range(2):
-                eng(dst[:, i, :, :, :, :], src[:, i, :, :, :, :])
-            ggrp[h, G] = t
 
-        def g_quant(h, G):
-            c, s = code_pair("gc%d%d" % (h, G), 512)
-            nc.vector.quantize_mx(out=c[:].bitcast(E5M2), scales=s[:], in_=ggrp[h, G][:])
-            gcodes[h, G] = (c, s)
+        def group_g(h, G, copy):
+            t = grouped_pool.tile([P, 2048], BF16, name="grouped", align_bytes=256)
+            dst = t[:].rearrange("p (r b i z s) -> p r b i z s", r=2, b=2, i=8, s=4)
+            src = raw_g[h][:, G, :, :].rearrange("p b (s i r z) -> p r b i z s", s=4, i=8, r=2)
+            for r in range(2):
+                if copy is on_gpsimd:
+                    for b in range(2):
+                        copy(dst[:, r, b, :, :, :], src[:, r, b, :, :, :])
+                else:
+                    copy(dst[:, r, :, :, :, :], src[:, r, :, :, :, :])
+            grouped_g[h, G] = t
 
-        def g_transpose(h, G, eng):
-            t = grp.tile([P, 2048], BF16, name="grp", align_bytes=256)
-            view = ggrp[h, G][:].rearrange("p (i k e j) -> p i e j k", i=2, e=2, j=4)
-            for jo in range(4):
-                ps = ps_mm.tile([P, 4, P], BF16, name="mm")
-                for tt in range(4):
-                    nc.tensor.transpose(ps[:, tt, :], view[:, tt // 2, tt % 2, jo, :], ident_b[:])
-                eng(t[:, jo * 512 : (jo + 1) * 512].rearrange("p (m t) -> p m t", t=4), ps[:].rearrange("p t m -> p m t"))
-            gtgrp[h, G] = t
+        def quantise_g(h, G):
+            codes_g[h, G] = quantised("g%d%d" % (h, G), 512, E5M2)
+            quantise(codes_g[h, G], everything, grouped_g[h, G][:])
 
-        def gt_quant(h, G):
-            c, s = code_pair("tc%d%d" % (h, G), 512)
-            nc.vector.quantize_mx(out=c[:].bitcast(E5M2), scales=s[:], in_=gtgrp[h, G][:])
-            gtcodes[h, G] = (c, s)
+        def group_w(G, Q, copy):
+            t = grouped_pool.tile([P, 2048], BF16, name="grouped", align_bytes=256)
+            copy(
+                t[:].rearrange("p (j m s) -> p j m s", j=4, s=4),
+                raw_w[G][:, :, 512 * Q : 512 * Q + 512].rearrange("p s (m j) -> p j m s", j=4),
+            )
+            grouped_w[G, Q] = t
 
-        def w_inter(G, Q, eng=vcopy):
-            t = grp.tile([P, 2048], BF16, name="grp", align_bytes=256)
-            src = raw["w", G][:].rearrange("p (o c) -> p o c", o=4)[:, :, 512 * Q : 512 * Q + 512]
-            eng(t[:].rearrange("p (j m o) -> p j m o", j=4, o=4), src.rearrange("p o (m j) -> p j m o", j=4))
-            wgrp[G, Q] = t
+        def quantise_w(G, Q):
+            codes_w[G, Q] = quantised("w%d%d" % (G, Q), 512, E4M3)
+            quantise(codes_w[G, Q], everything, grouped_w[G, Q][:])
 
-        def w_quant(G, Q):
-            c, s = code_pair("wc%d%d" % (G, Q), 512)
-            nc.vector.quantize_mx(out=c[:].bitcast(E4M3), scales=s[:], in_=wgrp[G, Q][:])
-            wcodes[G, Q] = (c, s)
+
+        def transpose_g(h, G):
+            t = grouped_pool.tile([P, 2048], BF16, name="grouped", align_bytes=256)
+            src = grouped_g[h, G][:].rearrange("p (r k e s) -> p r e s k", r=2, e=2, s=4)
+            for s in range(4):
+                acc = mix_psum.tile([P, 4, P], BF16, name="mix")
+                for slot in range(4):
+                    nc.tensor.transpose(acc[:, slot, :], src[:, slot // 2, slot % 2, s, :], ident_bf16[:])
+                on_scalar(t[:, s * 512 : (s + 1) * 512].rearrange("p (m t) -> p m t", t=4), acc[:].rearrange("p t m -> p m t"))
+            grouped_gt[h, G] = t
+
+        def quantise_gt(h, G):
+            codes_gt[h, G] = quantised("gt%d%d" % (h, G), 512, E5M2)
+            quantise(codes_gt[h, G], everything, grouped_gt[h, G][:])
+
 
         def mask(u):
             Q, h, j = u
-            t = mkp.tile([P, 2048], BF16, name="mask", align_bytes=64)
             q = 4 * Q + j
+            t = mask_pool.tile([P, 2048], BF16, name="mask_tile", align_bytes=64)
             nc.vector.tensor_scalar(
                 out=t[:],
-                in0=raw["x", h, Q][:, j, :, :].rearrange("p b f -> p (b f)"),
-                scalar1=s4[:, q : q + 1],
-                scalar2=nb4[:, q : q + 1],
+                in0=raw_x[h, Q][:, j, :, :].rearrange("p b f -> p (b f)"),
+                scalar1=scale4[:, q : q + 1],
+                scalar2=minus_shift4[:, q : q + 1],
                 op0=ALU.mult,
                 op1=ALU.is_gt,
             )
-            mk[u] = t
+            masked[u] = t
 
-        def act(u):
+        def activate(u):
             Q, h, j = u
             q = 4 * Q + j
-            t = rpool.tile([P, 4, 4, P], F32, name="r", align_bytes=64)
-            src = raw["x", h, Q][:, j, :, :].rearrange("p b (m c k e) -> p e (b m) c k", m=8, c=4, e=4)
+            t = relu_pool.tile([P, 4, 4, P], F32, name="relu_tile", align_bytes=64)
+            src = raw_x[h, Q][:, j, :, :].rearrange("p b (i c k e) -> p e (b i) c k", i=8, c=4, e=4)
             for e in range(4):
                 nc.scalar.activation(
                     out=t[:, e, :, :].rearrange("p c (g k) -> p g c k", k=8),
                     in_=src[:, e, :, :, :],
                     func=ACT.Relu,
-                    bias=b4[:, q : q + 1],
-                    scale=s4[:, q : q + 1],
+                    bias=shift4[:, q : q + 1],
+                    scale=scale4[:, q : q + 1],
                 )
-            rt[u] = t
+            relu[u] = t
 
-        def p_transpose(u):
-            ps = ps_pt.tile([P, 4, P], F32, name="pt")
-            for t in range(4):
+        def pool(u):
+            acc = pool_psum.tile([P, 4, P], F32, name="pool_acc")
+            for slot in range(4):
+                r, e = slot // 2, slot % 2
                 for n in range(4):
+                    dh, dw = n // 2, n % 2
                     nc.tensor.matmul(
-                        out=ps[:, t, :],
-                        lhsT=rt[u][:, 2 * (t % 2) + n % 2, 2 * (t // 2) + n // 2, :],
-                        rhs=ident_f[:],
+                        out=acc[:, slot, :],
+                        lhsT=relu[u][:, 2 * e + dw, 2 * r + dh, :],
+                        rhs=ident_f32[:],
                         start=(n == 0),
                         stop=(n == 3),
                         is_transpose=True,
                     )
-            pts[u] = ps
+            pooled_sum[u] = acc
 
-        def p_evac(u):
-            t = pgp.tile([P, 512], BF16, name="pg", align_bytes=256)
-            nc.scalar.copy(out=t[:].rearrange("p (m t) -> p m t", t=4), in_=pts[u][:].rearrange("p t m -> p m t"))
-            pgs[u] = t
-
-        def p_quant(u):
+        def round_p(u):
             Q, h, j = u
-            if (h, Q) not in pcodes:
-                pcodes[h, Q] = code_pair("pc%d%d" % (h, Q), 512)
-            c, s = pcodes[h, Q]
-            cols = slice(j * P, (j + 1) * P)
-            nc.vector.quantize_mx(out=c[:, cols].bitcast(E4M3), scales=s[:, cols], in_=pgs[u][:])
+            if j % 2 == 0:
+                pooled[Q, h, j // 2] = pooled_pool.tile([P, 2, 512], BF16, name="pooled_tile", align_bytes=256)
+            dst = pooled[Q, h, j // 2][:, j % 2, :]
+            on_scalar(dst.rearrange("p (m t) -> p m t", t=4), pooled_sum[u][:].rearrange("p t m -> p m t"))
+
+        def quantise_p(Q, h, pair):
+            if pair == 0:
+                codes_p[h, Q] = quantised("p%d%d" % (h, Q), 512, E4M3)
+            quantise(codes_p[h, Q], slice(256 * pair, 256 * pair + 256), pooled[Q, h, pair][:].rearrange("p a f -> p (a f)"))
 
         def dp(u):
             Q, h, j = u
-            ps = ps_dp.tile([P, 512], F32, name="dp")
-            cols = slice(j * P, (j + 1) * P)
+            acc = dp_psum.tile([P, 512], F32, name="dp_acc")
             for G in range(2):
-                wc, ws = wcodes[G, Q]
-                gc, gs = gcodes[h, G]
-                nc.tensor.matmul_mx(
-                    out=ps[:],
-                    lhsT=wc[:, cols].bitcast(E4M3),
-                    lhsT_scale=ws[:, cols],
-                    rhs=gc[:].bitcast(E5M2),
-                    rhs_scale=gs[:],
-                    start=(G == 0),
-                    stop=(G == 1),
-                )
-            dps[u] = ps
+                multiply(acc[:], codes_w[G, Q], block(j), codes_g[h, G], G == 0, G == 1)
+            dp_sum[u] = acc
 
-        def c_out(u):
+        def dx(u):
             Q, h, j = u
             q = 4 * Q + j
-            ot = o0p.tile([P, 2048], F32, name="o0", align_bytes=64)
-            dst = ot[:].rearrange("p (g i d z w) -> p i d g z w", i=2, d=2, z=16, w=2)
-            msk = mk[u][:].rearrange("p (g i d z w) -> p i d g z w", i=2, d=2, z=16, w=2)
-            for i in range(2):
-                src = dps[u][:, i * 256 : (i + 1) * 256].rearrange("p (g z) -> p g z", z=16).unsqueeze(3).broadcast_to([P, 16, 16, 2])
+            t = dx_pool.tile([P, 2048], F32, name="dx_tile", align_bytes=64)
+            dst = t[:].rearrange("p (g r d z w) -> p r d g z w", r=2, d=2, z=16, w=2)
+            keep = masked[u][:].rearrange("p (g r d z w) -> p r d g z w", r=2, d=2, z=16, w=2)
+            for r in range(2):
+                src = dp_sum[u][:, r * 256 : (r + 1) * 256].rearrange("p (g z) -> p g z", z=16).unsqueeze(3)
                 for d in range(2):
                     nc.vector.scalar_tensor_tensor(
-                        out=dst[:, i, d, :, :, :],
-                        in0=src,
-                        scalar=s4[:, q : q + 1],
-                        in1=msk[:, i, d, :, :, :],
+                        out=dst[:, r, d, :, :, :],
+                        in0=src.broadcast_to([P, 16, 16, 2]),
+                        scalar=scale4[:, q : q + 1],
+                        in1=keep[:, r, d, :, :, :],
                         op0=ALU.mult,
                         op1=ALU.mult,
                     )
-            nc.sync.dma_start(
-                out=out_0[2 * h : 2 * h + 2, 512 * Q : 512 * Q + 512, :, :].rearrange("b (p j) y z -> p j b (y z)", j=4)[:, j, :, :],
-                in_=ot[:].rearrange("p (b f) -> p b f", b=2),
-            )
+            rows = out_0[2 * h : 2 * h + 2, 512 * Q : 512 * Q + 512, :, :].rearrange("b (m j) y z -> m j b (y z)", j=4)
+            nc.sync.dma_start(out=rows[:, j, :, :], in_=t[:].rearrange("p (b f) -> p b f", b=2))
 
-        def warm_pe(k, rhs):
-            for i in range(k):
-                nc.tensor.matmul(out=warm_ps[:], lhsT=ident_b[:], rhs=rhs, start=True, stop=True)
 
-        def out1(Q, G, jo, eng):
-            ps = ps_mm.tile([P, 512], F32, name="mm")
-            cols = slice(jo * P, (jo + 1) * P)
+        def dw(Q, n, copy):
+            G, s = n // 4, n % 4
+            acc = mix_psum.tile([P, 512], F32, name="mix")
             for h in range(2):
-                tcd, tsc = gtcodes[h, G]
-                pc, psc = pcodes[h, Q]
-                nc.tensor.matmul_mx(
-                    out=ps[:],
-                    lhsT=tcd[:, cols].bitcast(E5M2),
-                    lhsT_scale=tsc[:, cols],
-                    rhs=pc[:].bitcast(E4M3),
-                    rhs_scale=psc[:],
-                    start=(h == 0),
-                    stop=(h == 1),
-                )
-            if jo % 2 == 0:
-                o1[Q, G, jo // 2] = o1p.tile([P, 2, 512], F32, name="o1", align_bytes=64)
-            ot = o1[Q, G, jo // 2]
-            eng(ot[:, jo % 2, :].rearrange("p (m j) -> p m j", j=4), ps[:].rearrange("p (j m) -> p m j", j=4))
-            if jo % 2 == 1:
-                nc.sync.dma_start(
-                    out=out_1[512 * G : 512 * G + 512, 512 * Q : 512 * Q + 512, :, :].rearrange("(p j) c u v -> p j (c u v)", j=4)[:, jo - 1 : jo + 1, :],
-                    in_=ot[:],
-                )
+                multiply(acc[:], codes_gt[h, G], block(s), codes_p[h, Q], h == 0, h == 1)
+            if s % 2 == 0:
+                dw_tile[Q, n // 2] = dw_pool.tile([P, 2, 512], F32, name="dw_rows", align_bytes=64)
+            t = dw_tile[Q, n // 2]
+            copy(t[:, s % 2, :].rearrange("p (m j) -> p m j", j=4), acc[:].rearrange("p (j m) -> p m j", j=4))
+            if s % 2 == 1:
+                rows = out_1[512 * G : 512 * G + 512, 512 * Q : 512 * Q + 512, :, :].rearrange("(m s) c u v -> m s (c u v)", s=4)
+                nc.sync.dma_start(out=rows[:, s - 1 : s + 1, :], in_=t[:])
 
         units = [(Q, h, j) for Q in range(2) for h in range(2) for j in range(4)]
-        N = len(units)
+        last = len(units)
 
         with tc.manual_schedule():
-            pv = {}
-            def load_params():
-                for nm, ap in (("var", running_var), ("gamma", gamma), ("mean", running_mean), ("beta", beta)):
-                    t = const.tile([P, 2, 4], BF16, name="pv_" + nm)
-                    nc.scalar.dma_start(out=t[:], in_=ap.rearrange("(q p j) -> p q j", q=2, j=4))
-                    pv[nm] = t[:].rearrange("p q j -> p (q j)")
-            ident_f = const.tile([P, P], F32, name="ident_f", align_bytes=64)
-            ident_b = const.tile([P, P], BF16, name="ident_b", align_bytes=64)
-            make_identity(nc, ident_b[:])
-            make_identity(nc, ident_f[:])
-            ve = const.tile([P, 8], F32, name="ve")
-            sd = const.tile([P, 8], F32, name="sd")
-            rs = const.tile([P, 8], F32, name="rs")
-            s4 = const.tile([P, 8], F32, name="s4")
-            ms = const.tile([P, 8], F32, name="ms")
-            b4 = const.tile([P, 8], F32, name="b4")
-            nb4 = const.tile([P, 8], F32, name="nb4")
-            warm = const.tile([P, 8], F32, name="warm")
-            zero = const.tile([P, 512], BF16, name="zero", align_bytes=64)
-            nc.gpsimd.memset(zero[:], 0.0)
-            def consts():
-                nc.vector.tensor_scalar(out=ve[:], in0=pv["var"], scalar1=EPS, scalar2=None, op0=ALU.add)
-                nc.scalar.activation(out=sd[:], in_=ve[:], func=ACT.Sqrt)
-                nc.vector.reciprocal(out=rs[:], in_=sd[:])
-                nc.vector.scalar_tensor_tensor(out=s4[:], in0=pv["gamma"], scalar=0.25, in1=rs[:], op0=ALU.mult, op1=ALU.mult)
-                nc.vector.tensor_tensor(out=ms[:], in0=pv["mean"], in1=s4[:], op=ALU.mult)
-                nc.vector.scalar_tensor_tensor(out=b4[:], in0=pv["beta"], scalar=0.25, in1=ms[:], op0=ALU.mult, op1=ALU.subtract)
-                nc.vector.tensor_scalar(out=nb4[:], in0=b4[:], scalar1=-1.0, scalar2=None, op0=ALU.mult)
-            nc.vector.memset(warm[:], 1.0)
-            nc.scalar.activation(out=sd[:], in_=warm[:], func=ACT.Sqrt)
-            load_params()
+            params = {}
+            for name, vec in (("var", running_var), ("gamma", gamma), ("mean", running_mean), ("beta", beta)):
+                t = const.tile([P, 2, 4], BF16, name="param_" + name)
+                nc.scalar.dma_start(out=t[:], in_=vec.rearrange("(q m j) -> m q j", q=2, j=4))
+                params[name] = t[:].rearrange("p q j -> p (q j)")
             load_g(0)
-            load_x(0, 0)
-            load_w(0)
             load_w(1)
+            load_w(0)
+            load_x(0, 0)
             load_g(1)
             load_x(1, 0)
             load_x(0, 1)
             load_x(1, 1)
-            g_inter(0, 0)
-            g_inter(0, 1)
-            consts()
-            g_quant(0, 1)
-            g_transpose(0, 1, scopy)
-            g_quant(0, 0)
-            gt_quant(0, 1)
-            g_transpose(0, 0, scopy)
-            mask(units[1])
+
+            ident_bf16 = const.tile([P, P], BF16, name="ident_bf16", align_bytes=64)
+            ident_f32 = const.tile([P, P], F32, name="ident_f32", align_bytes=64)
+            make_identity(nc, ident_bf16[:])
+            make_identity(nc, ident_f32[:])
+
+            ones = const.tile([P, 8], F32, name="ones")
+            var_eps = const.tile([P, 8], F32, name="var_eps")
+            std = const.tile([P, 8], F32, name="std")
+            inv_std = const.tile([P, 8], F32, name="inv_std")
+            scale4 = const.tile([P, 8], F32, name="scale4")
+            mean_scale4 = const.tile([P, 8], F32, name="mean_scale4")
+            shift4 = const.tile([P, 8], F32, name="shift4")
+            minus_shift4 = const.tile([P, 8], F32, name="minus_shift4")
+            nc.vector.memset(ones[:], 1.0)
+            nc.scalar.activation(out=std[:], in_=ones[:], func=ACT.Sqrt)
+            nc.vector.tensor_scalar(out=var_eps[:], in0=params["var"], scalar1=EPS, scalar2=None, op0=ALU.add)
+            nc.scalar.activation(out=std[:], in_=var_eps[:], func=ACT.Sqrt)
+            nc.vector.reciprocal(out=inv_std[:], in_=std[:])
+            nc.vector.scalar_tensor_tensor(out=scale4[:], in0=params["gamma"], scalar=0.25, in1=inv_std[:], op0=ALU.mult, op1=ALU.mult)
+            nc.vector.tensor_tensor(out=mean_scale4[:], in0=params["mean"], in1=scale4[:], op=ALU.mult)
+            nc.vector.scalar_tensor_tensor(out=shift4[:], in0=params["beta"], scalar=0.25, in1=mean_scale4[:], op0=ALU.mult, op1=ALU.subtract)
+            nc.vector.tensor_scalar(out=minus_shift4[:], in0=shift4[:], scalar1=-1.0, scalar2=None, op0=ALU.mult)
+
+            group_g(0, 1, on_vector)
+            group_g(0, 0, on_scalar)
+            quantise_g(0, 0)
+            transpose_g(0, 0)
+            transpose_g(0, 1)
+            quantise_g(0, 1)
+            group_w(1, 0, on_vector)
+            quantise_w(1, 0)
+            group_w(0, 0, on_vector)
+            quantise_gt(0, 0)
+            quantise_gt(0, 1)
+            quantise_w(0, 0)
+            group_w(0, 1, on_scalar)
             mask(units[0])
-            w_inter(0, 0)
-            gt_quant(0, 0)
-            w_quant(0, 0)
-            w_inter(1, 0)
-            w_quant(1, 0)
-            warm_pe(4, gtgrp[0, 0][:, 0:512])
+            mask(units[1])
+            quantise_w(0, 1)
             dp(units[0])
-            act(units[0])
-            w_inter(0, 1, scopy)
-            g_inter(1, 0, scopy)
-            g_inter(1, 1, vcopy)
-            act(units[1])
-            p_transpose(units[0])
-            warm_pe(1, zero[:])
-            p_evac(units[0])
-            dp(units[1])
-            mask(units[2])
-            c_out(units[0])
-            g_quant(1, 1)
-            g_quant(1, 0)
-            act(units[2])
-            p_transpose(units[1])
-            warm_pe(1, zero[:])
-            p_evac(units[1])
-            dp(units[2])
-            mask(units[3])
-            c_out(units[1])
-            p_quant(units[0])
-            w_inter(1, 1, vcopy)
-            act(units[3])
-            p_transpose(units[2])
-            warm_pe(1, zero[:])
-            p_evac(units[2])
-            dp(units[3])
-            mask(units[4])
-            c_out(units[2])
-            p_quant(units[1])
-            g_transpose(1, 1, scopy)
-            act(units[4])
-            p_transpose(units[3])
-            warm_pe(1, zero[:])
-            p_evac(units[3])
-            dp(units[4])
-            mask(units[5])
-            c_out(units[3])
-            p_quant(units[2])
-            w_quant(0, 1)
-            act(units[5])
-            p_transpose(units[4])
-            warm_pe(1, zero[:])
-            p_evac(units[4])
-            dp(units[5])
-            mask(units[6])
-            c_out(units[4])
-            p_quant(units[3])
-            act(units[6])
-            p_transpose(units[5])
-            warm_pe(1, zero[:])
-            p_evac(units[5])
-            dp(units[6])
-            mask(units[7])
-            c_out(units[5])
-            p_quant(units[4])
-            act(units[7])
-            p_transpose(units[6])
-            warm_pe(1, zero[:])
-            p_evac(units[6])
-            dp(units[7])
-            mask(units[8])
-            c_out(units[6])
-            p_quant(units[5])
-            w_quant(1, 1)
-            act(units[8])
-            p_transpose(units[7])
-            warm_pe(1, zero[:])
-            p_evac(units[7])
-            dp(units[8])
-            mask(units[9])
-            c_out(units[7])
-            p_quant(units[6])
-            g_transpose(1, 0, scopy)
-            act(units[9])
-            p_transpose(units[8])
-            warm_pe(1, zero[:])
-            p_evac(units[8])
-            dp(units[9])
-            mask(units[10])
-            c_out(units[8])
-            p_quant(units[7])
-            gt_quant(1, 0)
-            act(units[10])
-            p_transpose(units[9])
-            warm_pe(1, zero[:])
-            p_evac(units[9])
-            dp(units[10])
-            mask(units[11])
-            c_out(units[9])
-            p_quant(units[8])
-            gt_quant(1, 1)
-            out1(0, 0, 0, scopy)
-            out1(0, 0, 1, vcopy)
-            out1(0, 0, 2, scopy)
-            act(units[11])
-            p_transpose(units[10])
-            warm_pe(1, zero[:])
-            p_evac(units[10])
-            dp(units[11])
-            mask(units[12])
-            c_out(units[10])
-            p_quant(units[9])
-            out1(0, 1, 2, vcopy)
-            out1(0, 1, 3, scopy)
-            act(units[12])
-            p_transpose(units[11])
-            warm_pe(1, zero[:])
-            p_evac(units[11])
-            dp(units[12])
-            mask(units[13])
-            c_out(units[11])
-            p_quant(units[10])
-            out1(0, 0, 3, vcopy)
-            act(units[13])
-            p_transpose(units[12])
-            warm_pe(1, zero[:])
-            p_evac(units[12])
-            dp(units[13])
-            mask(units[14])
-            c_out(units[12])
-            p_quant(units[11])
-            out1(0, 1, 0, scopy)
-            out1(0, 1, 1, scopy)
-            act(units[14])
-            p_transpose(units[13])
-            warm_pe(1, zero[:])
-            p_evac(units[13])
-            dp(units[14])
-            mask(units[15])
-            c_out(units[13])
-            p_quant(units[12])
-            act(units[15])
-            p_transpose(units[14])
-            warm_pe(1, zero[:])
-            p_evac(units[14])
-            dp(units[15])
-            c_out(units[14])
-            p_quant(units[13])
-            p_transpose(units[15])
-            warm_pe(1, zero[:])
-            p_evac(units[15])
-            c_out(units[15])
-            p_quant(units[14])
-            p_quant(units[15])
-            out1(1, 0, 0, scopy)
-            out1(1, 0, 1, vcopy)
-            out1(1, 0, 2, scopy)
-            out1(1, 0, 3, vcopy)
-            out1(1, 1, 0, scopy)
-            out1(1, 1, 1, vcopy)
-            out1(1, 1, 2, scopy)
-            out1(1, 1, 3, vcopy)
+            group_g(1, 1, on_gpsimd)
+
+            for n in range(last + 3):
+                if n < last:
+                    activate(units[n])
+                if 1 <= n <= last:
+                    pool(units[n - 1])
+                    round_p(units[n - 1])
+                if 1 <= n < last:
+                    dp(units[n])
+                if 1 <= n < last - 1:
+                    mask(units[n + 1])
+                if n >= 4 and n % 2 == 0:
+                    Q, h, j = units[n - 3]
+                    quantise_p(Q, h, j // 2)
+                if 1 <= n <= last:
+                    dx(units[n - 1])
+                if n == 1:
+                    group_w(1, 1, on_vector)
+                    group_g(1, 0, on_vector)
+                    quantise_w(1, 1)
+                if n == 2:
+                    quantise_g(1, 1)
+                if n == 3:
+                    quantise_g(1, 0)
+                    transpose_g(1, 0)
+                    transpose_g(1, 1)
+                if n == 5:
+                    quantise_gt(1, 0)
+                    quantise_gt(1, 1)
+                if 10 <= n < 18:
+                    dw(0, n - 10, on_scalar)
+            for n in range(8):
+                dw(1, n, on_vector if n % 2 else on_scalar)

from contextlib import ExitStack

import concourse.mybir as mybir
from concourse.masks import make_identity

F32 = mybir.dt.float32
BF16 = mybir.dt.bfloat16
U32 = mybir.dt.uint32
U8 = mybir.dt.uint8
E4M3 = mybir.dt.float8_e4m3fn_x4
E5M2 = mybir.dt.float8_e5m2_x4
ALU = mybir.AluOpType
ACT = mybir.ActivationFunctionType

FLOPS = 2 * 2 * 1024 * 1024 * 1024
EPS = 1e-5
P = 128


def tile_modelnew_v_kernel(tc, x, gamma, beta, running_mean, running_var, weight, grad_out, out_0, out_1):
    nc = tc.nc

    def on_scalar(out, in_):
        nc.scalar.copy(out=out, in_=in_)

    def on_vector(out, in_):
        nc.vector.tensor_copy(out=out, in_=in_)

    def on_gpsimd(out, in_):
        nc.gpsimd.tensor_scalar(out=out, in0=in_, scalar1=1.0, scalar2=0.0, op0=ALU.mult, op1=ALU.add)

    with ExitStack() as ctx:

        def sbuf(name, bufs):
            return ctx.enter_context(tc.tile_pool(name=name, bufs=bufs))

        def psum(name, bufs):
            return ctx.enter_context(tc.psum_pool(name=name, bufs=bufs))

        const = sbuf("const", 1)
        raw_pool = sbuf("raw_pool", 3)
        x_pool = sbuf("x_pool", 3)
        grouped_pool = sbuf("grouped_pool", 5)
        code_pool = sbuf("code_pool", 1)
        mask_pool = sbuf("mask_pool", 4)
        relu_pool = sbuf("relu_pool", 3)
        pooled_pool = sbuf("pooled_pool", 3)
        dx_pool = sbuf("dx_pool", 4)
        dw_pool = sbuf("dw_pool", 4)
        dp_psum = psum("dp_psum", 3)
        pool_psum = psum("pool_psum", 2)
        mix_psum = psum("mix_psum", 3)

        raw_g, raw_w, raw_x = {}, {}, {}
        grouped_g, grouped_w, grouped_gt = {}, {}, {}
        codes_g, codes_w, codes_gt, codes_p = {}, {}, {}, {}
        masked, relu, pooled_sum, pooled, dp_sum, dw_tile = {}, {}, {}, {}, {}, {}

        def quantised(name, width, fmt):
            codes = code_pool.tile([P, width], U32, name=name + "_codes", align_bytes=256)
            scales = code_pool.tile([P, width], U8, name=name + "_scales", align_bytes=256)
            return codes, scales, fmt

        def quantise(dst, cols, src):
            codes, scales, fmt = dst
            nc.vector.quantize_mx(out=codes[:, cols].bitcast(fmt), scales=scales[:, cols], in_=src)

        def multiply(acc, lhs, lhs_cols, rhs, start, stop):
            lhs_codes, lhs_scales, lhs_fmt = lhs
            rhs_codes, rhs_scales, rhs_fmt = rhs
            nc.tensor.matmul_mx(
                out=acc,
                lhsT=lhs_codes[:, lhs_cols].bitcast(lhs_fmt),
                lhsT_scale=lhs_scales[:, lhs_cols],
                rhs=rhs_codes[:].bitcast(rhs_fmt),
                rhs_scale=rhs_scales[:],
                start=start,
                stop=stop,
            )

        everything = slice(0, 512)

        def block(n):
            return slice(n * P, (n + 1) * P)


        def load_g(h):
            t = raw_pool.tile([P, 2, 2, 1024], BF16, name="raw", align_bytes=256)
            for G in range(2):
                nc.sync.dma_start(
                    out=t[:, G, :, :],
                    in_=grad_out[2 * h : 2 * h + 2, 512 * G : 512 * G + 512, :, :].rearrange("b (m s) y z -> m b (s y z)", s=4),
                )
            raw_g[h] = t

        def load_w(G):
            t = raw_pool.tile([P, 4, 1024], BF16, name="raw", align_bytes=256)
            nc.sync.dma_start(out=t[:], in_=weight[512 * G : 512 * G + 512, :, :, :].rearrange("(m s) c u v -> m s (c u v)", s=4))
            raw_w[G] = t

        def load_x(h, Q):
            t = x_pool.tile([P, 4, 2, 1024], BF16, name="x_tile", align_bytes=256)
            for b in range(2):
                nc.sync.dma_start(
                    out=t[:, :, b, :],
                    in_=x[2 * h + b, 512 * Q : 512 * Q + 512, :, :].rearrange("(m j) y z -> m j (y z)", j=4),
                )
            raw_x[h, Q] = t


        def group_g(h, G, copy):
            t = grouped_pool.tile([P, 2048], BF16, name="grouped", align_bytes=256)
            dst = t[:].rearrange("p (r b i z s) -> p r b i z s", r=2, b=2, i=8, s=4)
            src = raw_g[h][:, G, :, :].rearrange("p b (s i r z) -> p r b i z s", s=4, i=8, r=2)
            for r in range(2):
                if copy is on_gpsimd:
                    for b in range(2):
                        copy(dst[:, r, b, :, :, :], src[:, r, b, :, :, :])
                else:
                    copy(dst[:, r, :, :, :, :], src[:, r, :, :, :, :])
            grouped_g[h, G] = t

        def quantise_g(h, G):
            codes_g[h, G] = quantised("g%d%d" % (h, G), 512, E5M2)
            quantise(codes_g[h, G], everything, grouped_g[h, G][:])

        def group_w(G, Q, copy):
            t = grouped_pool.tile([P, 2048], BF16, name="grouped", align_bytes=256)
            copy(
                t[:].rearrange("p (j m s) -> p j m s", j=4, s=4),
                raw_w[G][:, :, 512 * Q : 512 * Q + 512].rearrange("p s (m j) -> p j m s", j=4),
            )
            grouped_w[G, Q] = t

        def quantise_w(G, Q):
            codes_w[G, Q] = quantised("w%d%d" % (G, Q), 512, E4M3)
            quantise(codes_w[G, Q], everything, grouped_w[G, Q][:])


        def transpose_g(h, G):
            t = grouped_pool.tile([P, 2048], BF16, name="grouped", align_bytes=256)
            src = grouped_g[h, G][:].rearrange("p (r k e s) -> p r e s k", r=2, e=2, s=4)
            for s in range(4):
                acc = mix_psum.tile([P, 4, P], BF16, name="mix")
                for slot in range(4):
                    nc.tensor.transpose(acc[:, slot, :], src[:, slot // 2, slot % 2, s, :], ident_bf16[:])
                on_scalar(t[:, s * 512 : (s + 1) * 512].rearrange("p (m t) -> p m t", t=4), acc[:].rearrange("p t m -> p m t"))
            grouped_gt[h, G] = t

        def quantise_gt(h, G):
            codes_gt[h, G] = quantised("gt%d%d" % (h, G), 512, E5M2)
            quantise(codes_gt[h, G], everything, grouped_gt[h, G][:])


        def mask(u):
            Q, h, j = u
            q = 4 * Q + j
            t = mask_pool.tile([P, 2048], BF16, name="mask_tile", align_bytes=64)
            nc.vector.tensor_scalar(
                out=t[:],
                in0=raw_x[h, Q][:, j, :, :].rearrange("p b f -> p (b f)"),
                scalar1=scale4[:, q : q + 1],
                scalar2=minus_shift4[:, q : q + 1],
                op0=ALU.mult,
                op1=ALU.is_gt,
            )
            masked[u] = t

        def activate(u):
            Q, h, j = u
            q = 4 * Q + j
            t = relu_pool.tile([P, 4, 4, P], F32, name="relu_tile", align_bytes=64)
            src = raw_x[h, Q][:, j, :, :].rearrange("p b (i c k e) -> p e (b i) c k", i=8, c=4, e=4)
            for e in range(4):
                nc.scalar.activation(
                    out=t[:, e, :, :].rearrange("p c (g k) -> p g c k", k=8),
                    in_=src[:, e, :, :, :],
                    func=ACT.Relu,
                    bias=shift4[:, q : q + 1],
                    scale=scale4[:, q : q + 1],
                )
            relu[u] = t

        def pool(u):
            acc = pool_psum.tile([P, 4, P], F32, name="pool_acc")
            for slot in range(4):
                r, e = slot // 2, slot % 2
                for n in range(4):
                    dh, dw = n // 2, n % 2
                    nc.tensor.matmul(
                        out=acc[:, slot, :],
                        lhsT=relu[u][:, 2 * e + dw, 2 * r + dh, :],
                        rhs=ident_f32[:],
                        start=(n == 0),
                        stop=(n == 3),
                        is_transpose=True,
                    )
            pooled_sum[u] = acc

        def round_p(u):
            Q, h, j = u
            if j % 2 == 0:
                pooled[Q, h, j // 2] = pooled_pool.tile([P, 2, 512], BF16, name="pooled_tile", align_bytes=256)
            dst = pooled[Q, h, j // 2][:, j % 2, :]
            on_scalar(dst.rearrange("p (m t) -> p m t", t=4), pooled_sum[u][:].rearrange("p t m -> p m t"))

        def quantise_p(Q, h, pair):
            if pair == 0:
                codes_p[h, Q] = quantised("p%d%d" % (h, Q), 512, E4M3)
            quantise(codes_p[h, Q], slice(256 * pair, 256 * pair + 256), pooled[Q, h, pair][:].rearrange("p a f -> p (a f)"))

        def dp(u):
            Q, h, j = u
            acc = dp_psum.tile([P, 512], F32, name="dp_acc")
            for G in range(2):
                multiply(acc[:], codes_w[G, Q], block(j), codes_g[h, G], G == 0, G == 1)
            dp_sum[u] = acc

        def dx(u):
            Q, h, j = u
            q = 4 * Q + j
            t = dx_pool.tile([P, 2048], F32, name="dx_tile", align_bytes=64)
            dst = t[:].rearrange("p (g r d z w) -> p r d g z w", r=2, d=2, z=16, w=2)
            keep = masked[u][:].rearrange("p (g r d z w) -> p r d g z w", r=2, d=2, z=16, w=2)
            for r in range(2):
                src = dp_sum[u][:, r * 256 : (r + 1) * 256].rearrange("p (g z) -> p g z", z=16).unsqueeze(3)
                for d in range(2):
                    nc.vector.scalar_tensor_tensor(
                        out=dst[:, r, d, :, :, :],
                        in0=src.broadcast_to([P, 16, 16, 2]),
                        scalar=scale4[:, q : q + 1],
                        in1=keep[:, r, d, :, :, :],
                        op0=ALU.mult,
                        op1=ALU.mult,
                    )
            rows = out_0[2 * h : 2 * h + 2, 512 * Q : 512 * Q + 512, :, :].rearrange("b (m j) y z -> m j b (y z)", j=4)
            nc.sync.dma_start(out=rows[:, j, :, :], in_=t[:].rearrange("p (b f) -> p b f", b=2))


        def dw(Q, n, copy):
            G, s = n // 4, n % 4
            acc = mix_psum.tile([P, 512], F32, name="mix")
            for h in range(2):
                multiply(acc[:], codes_gt[h, G], block(s), codes_p[h, Q], h == 0, h == 1)
            if s % 2 == 0:
                dw_tile[Q, n // 2] = dw_pool.tile([P, 2, 512], F32, name="dw_rows", align_bytes=64)
            t = dw_tile[Q, n // 2]
            copy(t[:, s % 2, :].rearrange("p (m j) -> p m j", j=4), acc[:].rearrange("p (j m) -> p m j", j=4))
            if s % 2 == 1:
                rows = out_1[512 * G : 512 * G + 512, 512 * Q : 512 * Q + 512, :, :].rearrange("(m s) c u v -> m s (c u v)", s=4)
                nc.sync.dma_start(out=rows[:, s - 1 : s + 1, :], in_=t[:])

        units = [(Q, h, j) for Q in range(2) for h in range(2) for j in range(4)]
        last = len(units)

        with tc.manual_schedule():
            params = {}
            for name, vec in (("var", running_var), ("gamma", gamma), ("mean", running_mean), ("beta", beta)):
                t = const.tile([P, 2, 4], BF16, name="param_" + name)
                nc.scalar.dma_start(out=t[:], in_=vec.rearrange("(q m j) -> m q j", q=2, j=4))
                params[name] = t[:].rearrange("p q j -> p (q j)")
            load_g(0)
            load_w(1)
            load_w(0)
            load_x(0, 0)
            load_g(1)
            load_x(1, 0)
            load_x(0, 1)
            load_x(1, 1)

            ident_bf16 = const.tile([P, P], BF16, name="ident_bf16", align_bytes=64)
            ident_f32 = const.tile([P, P], F32, name="ident_f32", align_bytes=64)
            make_identity(nc, ident_bf16[:])
            make_identity(nc, ident_f32[:])

            ones = const.tile([P, 8], F32, name="ones")
            var_eps = const.tile([P, 8], F32, name="var_eps")
            std = const.tile([P, 8], F32, name="std")
            inv_std = const.tile([P, 8], F32, name="inv_std")
            scale4 = const.tile([P, 8], F32, name="scale4")
            mean_scale4 = const.tile([P, 8], F32, name="mean_scale4")
            shift4 = const.tile([P, 8], F32, name="shift4")
            minus_shift4 = const.tile([P, 8], F32, name="minus_shift4")
            nc.vector.memset(ones[:], 1.0)
            nc.scalar.activation(out=std[:], in_=ones[:], func=ACT.Sqrt)
            nc.vector.tensor_scalar(out=var_eps[:], in0=params["var"], scalar1=EPS, scalar2=None, op0=ALU.add)
            nc.scalar.activation(out=std[:], in_=var_eps[:], func=ACT.Sqrt)
            nc.vector.reciprocal(out=inv_std[:], in_=std[:])
            nc.vector.scalar_tensor_tensor(out=scale4[:], in0=params["gamma"], scalar=0.25, in1=inv_std[:], op0=ALU.mult, op1=ALU.mult)
            nc.vector.tensor_tensor(out=mean_scale4[:], in0=params["mean"], in1=scale4[:], op=ALU.mult)
            nc.vector.scalar_tensor_tensor(out=shift4[:], in0=params["beta"], scalar=0.25, in1=mean_scale4[:], op0=ALU.mult, op1=ALU.subtract)
            nc.vector.tensor_scalar(out=minus_shift4[:], in0=shift4[:], scalar1=-1.0, scalar2=None, op0=ALU.mult)

            group_g(0, 1, on_vector)
            group_g(0, 0, on_scalar)
            quantise_g(0, 0)
            transpose_g(0, 0)
            transpose_g(0, 1)
            quantise_g(0, 1)
            group_w(1, 0, on_vector)
            quantise_w(1, 0)
            group_w(0, 0, on_vector)
            quantise_gt(0, 0)
            quantise_gt(0, 1)
            quantise_w(0, 0)
            group_w(0, 1, on_scalar)
            mask(units[0])
            mask(units[1])
            quantise_w(0, 1)
            dp(units[0])
            group_g(1, 1, on_gpsimd)

            for n in range(last + 3):
                if n < last:
                    activate(units[n])
                if 1 <= n <= last:
                    pool(units[n - 1])
                    round_p(units[n - 1])
                if 1 <= n < last:
                    dp(units[n])
                if 1 <= n < last - 1:
                    mask(units[n + 1])
                if n >= 4 and n % 2 == 0:
                    Q, h, j = units[n - 3]
                    quantise_p(Q, h, j // 2)
                if 1 <= n <= last:
                    dx(units[n - 1])
                if n == 1:
                    group_w(1, 1, on_vector)
                    group_g(1, 0, on_vector)
                    quantise_w(1, 1)
                if n == 2:
                    quantise_g(1, 1)
                if n == 3:
                    quantise_g(1, 0)
                    transpose_g(1, 0)
                    transpose_g(1, 1)
                if n == 5:
                    quantise_gt(1, 0)
                    quantise_gt(1, 1)
                if 10 <= n < 18:
                    dw(0, n - 10, on_scalar)
            for n in range(8):
                dw(1, n, on_vector if n % 2 else on_scalar)
